import numpy as np
import ml_dtypes


def mxq(x, axis, fmt="e4m3"):
    dtype, down = {"e4m3": (ml_dtypes.float8_e4m3fn, 7), "e5m2": (ml_dtypes.float8_e5m2, 14)}[fmt]
    v = np.moveaxis(np.asarray(x, np.float32).astype(ml_dtypes.bfloat16).astype(np.float64), axis, -1)
    blocks = v.reshape(v.shape[:-1] + (-1, 32))
    amax = np.abs(blocks).max(-1, keepdims=True)
    byte = np.maximum(np.where(amax > 0, np.frexp(amax)[1] - 1 + 127, 0) - down, 1)
    scale = np.exp2(byte - 127.0)
    codes = (blocks / scale).astype(np.float32).astype(dtype).astype(np.float64)
    return np.moveaxis((codes * scale).reshape(v.shape), -1, axis)


WIDE = False


def mx_kscale(k):
    if not WIDE:
        return np.ones(k)
    levels = np.array([10, -10, 5, -5, 0])
    if k % 512:
        return np.exp2(np.random.permutation(np.resize(levels, k // 32))).repeat(32)
    a = np.empty((k // 512, 16))
    for p in range(k // 512):
        a[p, :8] = np.random.permutation(np.resize(levels, 8))
        for g in range(8):
            far = levels[np.abs(levels - a[p, g]) >= 10]
            a[p, g + 8] = far[np.random.randint(len(far))]
    return np.exp2(a.ravel()).repeat(32)


BF16 = ml_dtypes.bfloat16


def bf(x):
    return np.asarray(x, np.float32).astype(BF16)


def f64(x):
    return np.asarray(x).astype(np.float64)


B, S, HID, QK, H, C = 2, 1024, 1024, 1024, 8, 512
DK, DV = QK // H, HID // H
GFAST, GSLOW = 0.96875, 0.99609375


def setup_inputs():
    s = mx_kscale(S)
    lg = np.linspace(np.log(1.0 - GFAST), np.log(1.0 - GSLOW), H) + 0.3 * (np.random.random_sample(H) - 0.5)
    return {"q": bf(np.random.standard_normal((B, H, S, DK)) / DK ** 0.25),
            "k": bf(np.random.standard_normal((B, H, S, DK)) / DK ** 0.25 * s[:, None]),
            "v": bf(np.random.standard_normal((B, H, S, DV)) * 0.5 / s[:, None]),
            "gamma": bf(1.0 - np.exp(lg))}


def reference(q, k, v, gamma):
    q, k, g = f64(q), f64(k), f64(gamma)
    vq = mxq(f64(v), 2, "e4m3")
    idx = f64(np.arange(S))
    ret = np.zeros((B, H, S, DV))
    for i in range(S // C):
        r0, e = i * C, (i + 1) * C
        diff = idx[r0:e, None] - idx[None, :e]
        expn = np.maximum(diff, 0.0)
        dmask = np.where(diff >= 0, g[:, None, None] ** expn, 0.0)
        sc = (q[:, :, r0:e] @ k[:, :, :e].transpose(0, 1, 3, 2)) * dmask[None]
        ret[:, :, r0:e] = mxq(sc, 3, "e4m3") @ vq[:, :, :e]
    return ret

@@ -1,0 +1,283 @@
+from contextlib import ExitStack
+
+import concourse.mybir as mybir
+from concourse.masks import make_identity
+
+BF16 = mybir.dt.bfloat16
+F32 = mybir.dt.float32
+I32 = mybir.dt.int32
+U32 = mybir.dt.uint32
+U8 = mybir.dt.uint8
+FP8X4 = mybir.dt.float8_e4m3fn_x4
+ALU = mybir.AluOpType
+ACT = mybir.ActivationFunctionType
+
+B, H, S, D = 2, 8, 1024, 128
+HEADS = B * H
+P = 128
+PACK = 4
+ROWS = P * PACK
+CHUNKS = S // ROWS
+TILES = S // P
+UNIT = P * PACK
+
+DIAG0, PAST, DIAG1 = 0, 1, 2
+GROUPS = ((0, 0), (1, 0), (1, 1))
+V_UNITS = [(DIAG0, s) for s in range(PACK)] + [(PAST, s) for s in range(PACK)]
+G_UNITS = [(DIAG1, s) for s in range(PACK)]
+NV, NG = len(V_UNITS), len(G_UNITS)
+V_BANKS, G_BANKS = 3, 2
+
+REACH = PACK - 1
+SPAN = S + PACK
+FAR = 1e30
+
+FLOPS = B * H * 2 * 2 * D * (512 * 512 + 512 * 1024)
+
+
+def tile_multiscaleretention_pa_kernel(tc, q, k, v, gamma, out):
+    nc = tc.nc
+
+    with ExitStack() as ctx:
+        const = ctx.enter_context(tc.tile_pool(name="const", bufs=1))
+        tables = ctx.enter_context(tc.tile_pool(name="tables", bufs=2))
+        loads = ctx.enter_context(tc.tile_pool(name="loads", bufs=3))
+        operands = ctx.enter_context(tc.tile_pool(name="operands", bufs=2))
+        quantised = ctx.enter_context(tc.tile_pool(name="quantised", bufs=2))
+        staging = ctx.enter_context(tc.tile_pool(name="staging", bufs=3))
+        transposed_psum = ctx.enter_context(tc.psum_pool(name="transposed_psum", bufs=1))
+        v_psum = ctx.enter_context(tc.psum_pool(name="v_psum", bufs=V_BANKS))
+        g_psum = ctx.enter_context(tc.psum_pool(name="g_psum", bufs=G_BANKS))
+        out_psum = ctx.enter_context(tc.psum_pool(name="out_psum", bufs=1))
+        ctx.enter_context(tc.manual_schedule())
+
+        raw, turned, kT, qT, v_mx, decay, grouped, score_mx = {}, {}, {}, {}, {}, {}, {}, {}
+        v_bank, g_bank, staged, accs = {}, {}, {}, {}
+
+        def load(i):
+            h, b = divmod(i, B)
+            tiles = []
+            for name, src in (("k", k), ("q", q), ("v", v)):
+                t = loads.tile([P, TILES, D], BF16, name="raw_" + name)
+                nc.sync.dma_start(
+                    out=t[:].rearrange("p (g t) d -> p g t d", t=PACK),
+                    in_=src[b, h].rearrange("(g p t) d -> p g t d", p=P, t=PACK),
+                )
+                tiles.append(t)
+            raw[i] = tiles
+
+        def decay_table(h):
+            table = tables.tile([P, SPAN], F32, name="table")
+            nc.scalar.activation(
+                out=table[:], in_=distance[:], func=ACT.Exp, scale=ln_gamma[:, h : h + 1]
+            )
+            decay[h] = table
+
+        def transpose(i, which):
+            ps = transposed_psum.tile([P, TILES, P], BF16, name="turned")
+            for j in range(TILES):
+                nc.tensor.transpose(ps[:, j, :], raw[i][which][:, j, :], identity[:])
+            turned[(i, which)] = ps
+
+        def copy_transposed(i, which):
+            sb = operands.tile([P, TILES, P], BF16, name="kT" if which == 0 else "qT")
+            nc.scalar.copy(out=sb[:], in_=turned[(i, which)][:])
+            (kT if which == 0 else qT)[i] = sb
+
+        def regroup_v(i):
+            v_sb = raw[i][2]
+            t = operands.tile([P, CHUNKS * D * PACK], BF16, name="v_grouped", align_bytes=64)
+            nc.scalar.copy(
+                out=t[:].rearrange("p (g d w) -> p g d w", g=CHUNKS, w=PACK),
+                in_=v_sb[:].rearrange("p (g t) d -> p g d t", t=PACK)[:, :, :, ::-1],
+            )
+            v_mx[i] = t
+
+        def quantise_v(i):
+            codes = quantised.tile([P, CHUNKS * D], U32, name="v_codes", align_bytes=64)
+            scales = quantised.tile([P, CHUNKS * D], U8, name="v_scales", align_bytes=64)
+            nc.vector.quantize_mx(out=codes[:].bitcast(FP8X4), scales=scales[:], in_=v_mx[i][:])
+            v_mx[i] = (codes, scales)
+
+        def scores(bank, i, group, s):
+            chunk, g = GROUPS[group]
+            for w in range(PACK):
+                nc.tensor.matmul(
+                    bank[:, w, :],
+                    lhsT=kT[i][:, PACK * g + PACK - 1 - w, :],
+                    rhs=qT[i][:, PACK * chunk + s, :],
+                    start=True,
+                    stop=True,
+                )
+
+        def fill_v(n):
+            if n < HEADS * NV:
+                v_bank[n] = v_psum.tile([P, PACK, P], F32, name="v_scores")
+                scores(v_bank[n], n // NV, *V_UNITS[n % NV])
+
+        def fill_g(n):
+            if n < HEADS * NG:
+                g_bank[n] = g_psum.tile([P, PACK, P], F32, name="g_scores")
+                scores(g_bank[n], n // NG, *G_UNITS[n % NG])
+
+        def weights(i, group, s):
+            chunk, g = GROUPS[group]
+            first = ROWS * (chunk - g) + s
+            return decay[i // B][:, first : first + UNIT]
+
+        def masked(i, group, s):
+            if (i, group) not in grouped:
+                grouped[(i, group)] = quantised.tile(
+                    [P, PACK, UNIT], BF16, name="grouped%d" % group, align_bytes=64
+                )
+            return grouped[(i, group)][:, s, :]
+
+        def mask_v(n):
+            i = n // NV
+            group, s = V_UNITS[n % NV]
+            nc.vector.tensor_tensor(
+                out=masked(i, group, s).rearrange("p (c w) -> p c w", w=PACK),
+                in0=v_bank[n][:].rearrange("p w c -> p c w"),
+                in1=weights(i, group, s).rearrange("p (c w) -> p c w", w=PACK),
+                op=ALU.mult,
+            )
+
+        def drain_g(n):
+            if n < HEADS * NG:
+                staged[n] = staging.tile([P, UNIT], F32, name="staged")
+                nc.scalar.copy(
+                    out=staged[n][:].rearrange("p (c w) -> p c w", w=PACK),
+                    in_=g_bank[n][:].rearrange("p w c -> p c w"),
+                )
+
+        def mask_g(n):
+            i = n // NG
+            group, s = G_UNITS[n % NG]
+            nc.gpsimd.tensor_tensor(
+                out=masked(i, group, s), in0=staged[n][:], in1=weights(i, group, s), op=ALU.mult
+            )
+
+        def quantise(i, group):
+            codes = quantised.tile([P, ROWS], U32, name="codes%d" % group, align_bytes=64)
+            scales = quantised.tile([P, ROWS], U8, name="scales%d" % group, align_bytes=64)
+            nc.vector.quantize_mx(
+                out=codes[:].bitcast(FP8X4),
+                scales=scales[:],
+                in_=grouped[(i, group)][:].rearrange("p s e -> p (s e)"),
+            )
+            score_mx[(i, group)] = (codes, scales)
+
+        def retention(i, chunk):
+            v_codes, v_scales = v_mx[i]
+            groups = [group for group in (DIAG0, PAST, DIAG1) if GROUPS[group][0] == chunk]
+            acc = out_psum.tile([P, PACK, D], F32, name="acc%d" % chunk)
+            for s in range(PACK):
+                for group in groups:
+                    g = GROUPS[group][1]
+                    codes, scales = score_mx[(i, group)]
+                    nc.tensor.matmul_mx(
+                        out=acc[:, s, :],
+                        lhsT=codes[:, s * P : (s + 1) * P].bitcast(FP8X4),
+                        lhsT_scale=scales[:, s * P : (s + 1) * P],
+                        rhs=v_codes[:, g * D : (g + 1) * D].bitcast(FP8X4),
+                        rhs_scale=v_scales[:, g * D : (g + 1) * D],
+                        start=(group == groups[0]),
+                        stop=(group == groups[-1]),
+                    )
+            accs[(i, chunk)] = acc
+
+        def store(i, chunk):
+            h, b = divmod(i, B)
+            out_sb = staging.tile([P, PACK, D], F32, name="out_sb")
+            nc.scalar.copy(out=out_sb[:], in_=accs[(i, chunk)][:])
+            rows = out[b, h, chunk * ROWS : (chunk + 1) * ROWS, :]
+            nc.sync.dma_start(out=rows.rearrange("(c s) d -> c s d", s=PACK), in_=out_sb[:])
+
+        gamma_bf = const.tile([P, H], BF16)
+        nc.sync.dma_start(out=gamma_bf[:], in_=gamma.partition_broadcast(P))
+        load(0)
+        load(1)
+
+        ln_gamma = const.tile([P, H], F32)
+        nc.scalar.activation(out=ln_gamma[:], in_=gamma_bf[:], func=ACT.Ln)
+        nc.vector.tensor_scalar_min(out=ln_gamma[:], in0=ln_gamma[:], scalar1=-1e-25)
+
+        identity = const.tile([P, P], BF16)
+        make_identity(nc, identity[:])
+        steps = const.tile([P, SPAN], I32)
+        nc.gpsimd.iota(steps[:], pattern=[[1, SPAN]], base=-REACH, channel_multiplier=-PACK)
+        behind = const.tile([P, SPAN], F32)
+        nc.vector.tensor_scalar(
+            out=behind[:], in0=steps[:], scalar1=0.0, scalar2=FAR, op0=ALU.is_lt, op1=ALU.mult
+        )
+        distance = const.tile([P, SPAN], F32)
+        nc.vector.scalar_tensor_tensor(
+            out=distance[:], in0=steps[:], scalar=0.0, in1=behind[:], op0=ALU.max, op1=ALU.add
+        )
+
+        decay_table(0)
+        transpose(0, 0)
+        copy_transposed(0, 0)
+        transpose(0, 1)
+        copy_transposed(0, 1)
+        for n in range(V_BANKS):
+            fill_v(n)
+        for n in range(G_BANKS):
+            fill_g(n)
+        drain_g(0)
+        regroup_v(0)
+
+        for i in range(HEADS):
+            nxt = i + 1 < HEADS
+            if i + 2 < HEADS:
+                load(i + 2)
+            v0, g0 = i * NV, i * NG
+            if nxt:
+                transpose(i + 1, 0)
+                copy_transposed(i + 1, 0)
+            if i > 0:
+                retention(i - 1, 1)
+            mask_g(g0)
+            drain_g(g0 + 1)
+            mask_v(v0)
+            fill_v(v0 + 3)
+            mask_v(v0 + 1)
+            fill_v(v0 + 4)
+            mask_g(g0 + 1)
+            fill_g(g0 + 2)
+            drain_g(g0 + 2)
+            mask_v(v0 + 2)
+            fill_v(v0 + 5)
+            if nxt:
+                transpose(i + 1, 1)
+                copy_transposed(i + 1, 1)
+            mask_v(v0 + 3)
+            fill_v(v0 + 6)
+            mask_g(g0 + 2)
+            fill_g(g0 + 3)
+            drain_g(g0 + 3)
+            if i > 0:
+                store(i - 1, 0)
+            mask_v(v0 + 4)
+            fill_v(v0 + 7)
+            mask_g(g0 + 3)
+            if i > 0:
+                store(i - 1, 1)
+            if nxt:
+                regroup_v(i + 1)
+                if (i + 1) % B == 0:
+                    decay_table((i + 1) // B)
+            for x in range(5, 8):
+                mask_v(v0 + x)
+                fill_v(v0 + x + V_BANKS)
+            fill_g(g0 + NG)
+            fill_g(g0 + NG + 1)
+            drain_g(g0 + NG)
+            quantise_v(i)
+            quantise(i, DIAG0)
+            quantise(i, PAST)
+            retention(i, 0)
+            quantise(i, DIAG1)
+        retention(HEADS - 1, 1)
+        store(HEADS - 1, 0)
+        store(HEADS - 1, 1)

@@ -23,8 +23,8 @@ UNIT = P * PACK
 
 DIAG0, PAST, DIAG1 = 0, 1, 2
 GROUPS = ((0, 0), (1, 0), (1, 1))
-V_UNITS = [(DIAG0, s) for s in range(PACK)] + [(PAST, s) for s in range(PACK)]
-G_UNITS = [(DIAG1, s) for s in range(PACK)]
+G_UNITS = [(DIAG1, s) for s in range(3)]
+V_UNITS = [(DIAG1, 3)] + [(group, s) for group in (DIAG0, PAST) for s in range(PACK)]
 NV, NG = len(V_UNITS), len(G_UNITS)
 V_BANKS, G_BANKS = 3, 2
 
@@ -224,7 +224,7 @@ def tile_multiscaleretention_pa_kernel(tc, q, k, v, gamma, out):
             fill_v(n)
         for n in range(G_BANKS):
             fill_g(n)
-        drain_g(0)
+            drain_g(n)
         regroup_v(0)
 
         for i in range(HEADS):
@@ -232,47 +232,44 @@ def tile_multiscaleretention_pa_kernel(tc, q, k, v, gamma, out):
             if i + 2 < HEADS:
                 load(i + 2)
             v0, g0 = i * NV, i * NG
+
+            def step(x):
+                mask_v(v0 + x)
+                fill_v(v0 + x + V_BANKS)
+
             if nxt:
                 transpose(i + 1, 0)
                 copy_transposed(i + 1, 0)
             if i > 0:
                 retention(i - 1, 1)
-            mask_g(g0)
-            drain_g(g0 + 1)
-            mask_v(v0)
-            fill_v(v0 + 3)
-            mask_v(v0 + 1)
-            fill_v(v0 + 4)
-            mask_g(g0 + 1)
-            fill_g(g0 + 2)
-            drain_g(g0 + 2)
-            mask_v(v0 + 2)
-            fill_v(v0 + 5)
+            for j in range(NG):
+                mask_g(g0 + j)
+                if j == 0:
+                    fill_g(g0 + 2)
+                    drain_g(g0 + 2)
+            step(0)
+            step(1)
+            step(2)
             if nxt:
                 transpose(i + 1, 1)
                 copy_transposed(i + 1, 1)
-            mask_v(v0 + 3)
-            fill_v(v0 + 6)
-            mask_g(g0 + 2)
-            fill_g(g0 + 3)
-            drain_g(g0 + 3)
+            step(3)
+            step(4)
+            step(5)
+            fill_g(g0 + NG)
+            fill_g(g0 + NG + 1)
+            step(6)
+            step(7)
+            step(8)
             if i > 0:
                 store(i - 1, 0)
-            mask_v(v0 + 4)
-            fill_v(v0 + 7)
-            mask_g(g0 + 3)
-            if i > 0:
                 store(i - 1, 1)
             if nxt:
                 regroup_v(i + 1)
                 if (i + 1) % B == 0:
                     decay_table((i + 1) // B)
-            for x in range(5, 8):
-                mask_v(v0 + x)
-                fill_v(v0 + x + V_BANKS)
-            fill_g(g0 + NG)
-            fill_g(g0 + NG + 1)
             drain_g(g0 + NG)
+            drain_g(g0 + NG + 1)
             quantise_v(i)
             quantise(i, DIAG0)
             quantise(i, PAST)

@@ -15,21 +15,23 @@ ACT = mybir.ActivationFunctionType
 B, H, S, D = 2, 8, 1024, 128
 HEADS = B * H
 P = 128
+HALF = P // 2
 PACK = 4
 ROWS = P * PACK
 CHUNKS = S // ROWS
 TILES = S // P
 UNIT = P * PACK
+STRIP = UNIT // 2
 
-DIAG0, PAST, DIAG1 = 0, 1, 2
-GROUPS = ((0, 0), (1, 0), (1, 1))
-G_UNITS = [(DIAG1, s) for s in range(3)]
-V_UNITS = [(DIAG1, 3)] + [(group, s) for group in (DIAG0, PAST) for s in range(PACK)]
+PACKED, LATE0, PAST, LATE1 = 0, 1, 2, 3
+V_UNITS = [(kind, x, e) for kind, x in ((PACKED, 0), (LATE0, 0), (PAST, 0), (PAST, 1)) for e in range(2)]
+G_UNITS = [(LATE1, 0, e) for e in range(2)]
 NV, NG = len(V_UNITS), len(G_UNITS)
 V_BANKS, G_BANKS = 3, 2
 
-REACH = PACK - 1
-SPAN = S + PACK
+WIDTH = STRIP + PACK
+PAST_AT = 3 * WIDTH
+TABLE = PAST_AT + UNIT
 FAR = 1e30
 
 FLOPS = B * H * 2 * 2 * D * (512 * 512 + 512 * 1024)
@@ -51,45 +53,88 @@ def tile_multiscaleretention_pa_kernel(tc, q, k, v, gamma, out):
         out_psum = ctx.enter_context(tc.psum_pool(name="out_psum", bufs=1))
         ctx.enter_context(tc.manual_schedule())
 
-        raw, turned, kT, qT, v_mx, decay, grouped, score_mx = {}, {}, {}, {}, {}, {}, {}, {}
-        v_bank, g_bank, staged, accs = {}, {}, {}, {}
+        raw, turned_k, turned_q, kT, qT, v_mx, decay = {}, {}, {}, {}, {}, {}, {}
+        v_bank, g_bank, staged, accs, grouped, score_mx = {}, {}, {}, {}, {}, {}
+
+        def load_keys(i, name, src):
+            h, b = divmod(i, B)
+            t = loads.tile([P, CHUNKS, PACK, D], BF16, name="raw_" + name)
+            for p0, p1, g, first in (
+                (0, P, 0, 0),
+                (0, HALF, 1, ROWS + ROWS // 2),
+                (HALF, P, 1, ROWS),
+            ):
+                nc.sync.dma_start(
+                    out=t[p0:p1, g, :, :],
+                    in_=src[b, h, first : first + PACK * (p1 - p0), :].rearrange(
+                        "(p t) d -> p t d", t=PACK
+                    ),
+                )
+            return t
 
         def load(i):
             h, b = divmod(i, B)
-            tiles = []
-            for name, src in (("k", k), ("q", q), ("v", v)):
-                t = loads.tile([P, TILES, D], BF16, name="raw_" + name)
-                nc.sync.dma_start(
-                    out=t[:].rearrange("p (g t) d -> p g t d", t=PACK),
-                    in_=src[b, h].rearrange("(g p t) d -> p g t d", p=P, t=PACK),
-                )
-                tiles.append(t)
-            raw[i] = tiles
-
-        def decay_table(h):
-            table = tables.tile([P, SPAN], F32, name="table")
-            nc.scalar.activation(
-                out=table[:], in_=distance[:], func=ACT.Exp, scale=ln_gamma[:, h : h + 1]
+            k_sb = load_keys(i, "k", k)
+            q_sb = loads.tile([P, CHUNKS, PACK, D], BF16, name="raw_q")
+            nc.sync.dma_start(
+                out=q_sb[:], in_=q[b, h].rearrange("(g p t) d -> p g t d", p=P, t=PACK)
             )
-            decay[h] = table
+            v_sb = load_keys(i, "v", v)
+            raw[i] = (k_sb, q_sb, v_sb)
 
-        def transpose(i, which):
-            ps = transposed_psum.tile([P, TILES, P], BF16, name="turned")
+        def decay_table(h, first, last):
+            if first == 0:
+                decay[h] = tables.tile([P, TABLE], F32, name="table")
+            nc.scalar.activation(
+                out=decay[h][:, first:last],
+                in_=distance[:, first:last],
+                func=ACT.Exp,
+                scale=ln_gamma[:, h : h + 1],
+            )
+
+        def transpose_k(i):
+            ps = transposed_psum.tile([P, PACK, CHUNKS * 2, HALF], BF16, name="turned")
+            for t in range(PACK):
+                for g in range(CHUNKS):
+                    nc.tensor.transpose(
+                        ps[:, t, 2 * g : 2 * g + 2, :].rearrange("p b c -> p (b c)"),
+                        raw[i][0][:, g, t, :],
+                        identity[:],
+                    )
+            turned_k[i] = ps
+
+        def transpose_q(i):
+            if i == 0:
+                ps = out_psum.tile([P, TILES, P], BF16, name="acc1")
+            else:
+                ps = transposed_psum.tile([P, TILES, P], BF16, name="turned")
             for j in range(TILES):
-                nc.tensor.transpose(ps[:, j, :], raw[i][which][:, j, :], identity[:])
-            turned[(i, which)] = ps
+                g, s = divmod(j, PACK)
+                nc.tensor.transpose(ps[:, j, :], raw[i][1][:, g, s, :], identity[:])
+            turned_q[i] = ps
 
-        def copy_transposed(i, which):
-            sb = operands.tile([P, TILES, P], BF16, name="kT" if which == 0 else "qT")
-            nc.scalar.copy(out=sb[:], in_=turned[(i, which)][:])
-            (kT if which == 0 else qT)[i] = sb
+        def copy_k(i):
+            sb = operands.tile([P, PACK, CHUNKS * 2, HALF], BF16, name="kT")
+            nc.scalar.copy(out=sb[:], in_=turned_k[i][:])
+            kT[i] = sb
+
+        def copy_k_padded(i):
+            nc.scalar.copy(out=padded_k[i % 2][:, :, ::3, :], in_=turned_k[i][:, :, ::3, :])
+
+        def copy_q(i):
+            sb = operands.tile([P, CHUNKS, 2, 2, P], BF16, name="qT")
+            copy = nc.vector.tensor_copy if i == 0 else nc.scalar.copy
+            copy(
+                out=sb[:].rearrange("p g a e c -> p (g a e c)"),
+                in_=turned_q[i][:].rearrange("p j c -> p (j c)"),
+            )
+            qT[i] = sb
 
         def regroup_v(i):
-            v_sb = raw[i][2]
             t = operands.tile([P, CHUNKS * D * PACK], BF16, name="v_grouped", align_bytes=64)
             nc.scalar.copy(
                 out=t[:].rearrange("p (g d w) -> p g d w", g=CHUNKS, w=PACK),
-                in_=v_sb[:].rearrange("p (g t) d -> p g d t", t=PACK)[:, :, :, ::-1],
+                in_=raw[i][2][:].rearrange("p g t d -> p g d t")[:, :, :, ::-1],
             )
             v_mx[i] = t
 
@@ -99,99 +144,158 @@ def tile_multiscaleretention_pa_kernel(tc, q, k, v, gamma, out):
             nc.vector.quantize_mx(out=codes[:].bitcast(FP8X4), scales=scales[:], in_=v_mx[i][:])
             v_mx[i] = (codes, scales)
 
-        def scores(bank, i, group, s):
-            chunk, g = GROUPS[group]
-            for w in range(PACK):
-                nc.tensor.matmul(
-                    bank[:, w, :],
-                    lhsT=kT[i][:, PACK * g + PACK - 1 - w, :],
-                    rhs=qT[i][:, PACK * chunk + s, :],
-                    start=True,
-                    stop=True,
+        def pad_v(i):
+            codes = v_mx[i][0]
+            for g, p0 in ((0, 0), (1, HALF)):
+                nc.vector.tensor_copy(
+                    out=padded_v[i % 2][p0 : p0 + HALF, g * D : (g + 1) * D].bitcast(I32),
+                    in_=codes[p0 : p0 + HALF, g * D : (g + 1) * D].bitcast(I32),
                 )
+
+        def fill(bank, i, kind, x, e):
+            def queries(chunk, half):
+                return qT[i][:, chunk, :, e, half * HALF : (half + 1) * HALF]
+
+            def keys(tile, t, first):
+                return tile[:, t, first : first + 2, :].rearrange("p b c -> p (b c)")
+
+            for w in range(PACK):
+                t = PACK - 1 - w
+                if kind == PACKED:
+                    terms = [
+                        (keys(padded_k[i % 2], t, 0), queries(0, 0)),
+                        (keys(padded_k[i % 2], t, 2), queries(1, 0)),
+                    ]
+                elif kind == LATE0:
+                    terms = [(keys(kT[i], t, 0), queries(0, 1))]
+                elif kind == LATE1:
+                    terms = [(keys(kT[i], t, 2), queries(1, 1))]
+                else:
+                    terms = [(keys(kT[i], t, 0), queries(1, x))]
+                for n, (lhsT, rhs) in enumerate(terms):
+                    nc.tensor.matmul(
+                        bank[:, w, :, :],
+                        lhsT=lhsT,
+                        rhs=rhs,
+                        start=(n == 0),
+                        stop=(n == len(terms) - 1),
+                    )
 
         def fill_v(n):
             if n < HEADS * NV:
-                v_bank[n] = v_psum.tile([P, PACK, P], F32, name="v_scores")
-                scores(v_bank[n], n // NV, *V_UNITS[n % NV])
+                v_bank[n] = v_psum.tile([P, PACK, 2, HALF], F32, name="v_scores")
+                fill(v_bank[n], n // NV, *V_UNITS[n % NV])
 
         def fill_g(n):
             if n < HEADS * NG:
-                g_bank[n] = g_psum.tile([P, PACK, P], F32, name="g_scores")
-                scores(g_bank[n], n // NG, *G_UNITS[n % NG])
+                g_bank[n] = g_psum.tile([P, PACK, 2, HALF], F32, name="g_scores")
+                fill(g_bank[n], n // NG, *G_UNITS[n % NG])
 
-        def weights(i, group, s):
-            chunk, g = GROUPS[group]
-            first = ROWS * (chunk - g) + s
-            return decay[i // B][:, first : first + UNIT]
+        def strip(i, kind, a, e):
+            first = (PACKED, LATE0, LATE1).index(kind) * WIDTH + 2 * a + e
+            return decay[i // B][:, first : first + STRIP]
 
-        def masked(i, group, s):
-            if (i, group) not in grouped:
-                grouped[(i, group)] = quantised.tile(
-                    [P, PACK, UNIT], BF16, name="grouped%d" % group, align_bytes=64
+        def masked(i, kind, x, e):
+            name = "late" if kind == LATE1 else "past" if kind == PAST else "early"
+            units = 2 if kind == LATE1 else 4
+            if (i, name) not in grouped:
+                grouped[(i, name)] = quantised.tile(
+                    [P, units, 2, STRIP], BF16, name="grouped_" + name, align_bytes=64
                 )
-            return grouped[(i, group)][:, s, :]
+            return grouped[(i, name)][:, 2 * (1 if kind == LATE0 else x) + e, :, :]
 
         def mask_v(n):
             i = n // NV
-            group, s = V_UNITS[n % NV]
-            nc.vector.tensor_tensor(
-                out=masked(i, group, s).rearrange("p (c w) -> p c w", w=PACK),
-                in0=v_bank[n][:].rearrange("p w c -> p c w"),
-                in1=weights(i, group, s).rearrange("p (c w) -> p c w", w=PACK),
-                op=ALU.mult,
-            )
+            kind, x, e = V_UNITS[n % NV]
+            dst = masked(i, kind, x, e)
+            if kind == PAST:
+                nc.vector.scalar_tensor_tensor(
+                    out=dst.rearrange("p a (c w) -> p a c w", w=PACK),
+                    in0=v_bank[n][:].rearrange("p w a c -> p a c w"),
+                    scalar=farther[:, i // B, 2 * x + e : 2 * x + e + 1],
+                    in1=decay[i // B][:, PAST_AT:TABLE].rearrange(
+                        "p (a c w) -> p a c w", a=2, w=PACK
+                    ),
+                    op0=ALU.mult,
+                    op1=ALU.mult,
+                )
+            else:
+                for a in range(2):
+                    nc.vector.tensor_tensor(
+                        out=dst[:, a, :].rearrange("p (c w) -> p c w", w=PACK),
+                        in0=v_bank[n][:, :, a, :].rearrange("p w c -> p c w"),
+                        in1=strip(i, kind, a, e).rearrange("p (c w) -> p c w", w=PACK),
+                        op=ALU.mult,
+                    )
 
         def drain_g(n):
             if n < HEADS * NG:
-                staged[n] = staging.tile([P, UNIT], F32, name="staged")
+                staged[n] = staging.tile([P, 2, STRIP], F32, name="staged")
                 nc.scalar.copy(
-                    out=staged[n][:].rearrange("p (c w) -> p c w", w=PACK),
-                    in_=g_bank[n][:].rearrange("p w c -> p c w"),
+                    out=staged[n][:].rearrange("p a (c w) -> p a c w", w=PACK),
+                    in_=g_bank[n][:].rearrange("p w a c -> p a c w"),
                 )
 
         def mask_g(n):
             i = n // NG
-            group, s = G_UNITS[n % NG]
-            nc.gpsimd.tensor_tensor(
-                out=masked(i, group, s), in0=staged[n][:], in1=weights(i, group, s), op=ALU.mult
-            )
+            kind, x, e = G_UNITS[n % NG]
+            dst = masked(i, kind, x, e)
+            for a in range(2):
+                nc.gpsimd.tensor_tensor(
+                    out=dst[:, a, :],
+                    in0=staged[n][:, a, :],
+                    in1=strip(i, kind, a, e),
+                    op=ALU.mult,
+                )
 
-        def quantise(i, group):
-            codes = quantised.tile([P, ROWS], U32, name="codes%d" % group, align_bytes=64)
-            scales = quantised.tile([P, ROWS], U8, name="scales%d" % group, align_bytes=64)
+        def quantise(i, name):
+            units = 2 if name == "late" else 4
+            codes = quantised.tile([P, units * P], U32, name="codes_" + name, align_bytes=64)
+            scales = quantised.tile([P, units * P], U8, name="scales_" + name, align_bytes=64)
             nc.vector.quantize_mx(
                 out=codes[:].bitcast(FP8X4),
                 scales=scales[:],
-                in_=grouped[(i, group)][:].rearrange("p s e -> p (s e)"),
+                in_=grouped[(i, name)][:].rearrange("p u a e -> p (u a e)"),
             )
-            score_mx[(i, group)] = (codes, scales)
+            score_mx[(i, name)] = (codes, scales)
 
         def retention(i, chunk):
             v_codes, v_scales = v_mx[i]
-            groups = [group for group in (DIAG0, PAST, DIAG1) if GROUPS[group][0] == chunk]
             acc = out_psum.tile([P, PACK, D], F32, name="acc%d" % chunk)
-            for s in range(PACK):
-                for group in groups:
-                    g = GROUPS[group][1]
-                    codes, scales = score_mx[(i, group)]
-                    nc.tensor.matmul_mx(
-                        out=acc[:, s, :],
-                        lhsT=codes[:, s * P : (s + 1) * P].bitcast(FP8X4),
-                        lhsT_scale=scales[:, s * P : (s + 1) * P],
-                        rhs=v_codes[:, g * D : (g + 1) * D].bitcast(FP8X4),
-                        rhs_scale=v_scales[:, g * D : (g + 1) * D],
-                        start=(group == groups[0]),
-                        stop=(group == groups[-1]),
-                    )
+            for x in range(2):
+                for e in range(2):
+                    slot = 2 * x + e
+                    if chunk == 0:
+                        passes = [("early", slot, padded_v[i % 2] if x == 0 else v_codes, 0)]
+                    elif x == 0:
+                        passes = [("past", slot, v_codes, 0), ("early", e, padded_v[i % 2], 1)]
+                    else:
+                        passes = [("past", slot, v_codes, 0), ("late", e, v_codes, 1)]
+                    for n, (name, unit, values, g) in enumerate(passes):
+                        codes, scales = score_mx[(i, name)]
+                        nc.tensor.matmul_mx(
+                            out=acc[:, slot, :],
+                            lhsT=codes[:, unit * P : (unit + 1) * P].bitcast(FP8X4),
+                            lhsT_scale=scales[:, unit * P : (unit + 1) * P],
+                            rhs=values[:, g * D : (g + 1) * D].bitcast(FP8X4),
+                            rhs_scale=v_scales[:, g * D : (g + 1) * D],
+                            start=(n == 0),
+                            stop=(n == len(passes) - 1),
+                        )
             accs[(i, chunk)] = acc
 
         def store(i, chunk):
             h, b = divmod(i, B)
-            out_sb = staging.tile([P, PACK, D], F32, name="out_sb")
-            nc.scalar.copy(out=out_sb[:], in_=accs[(i, chunk)][:])
-            rows = out[b, h, chunk * ROWS : (chunk + 1) * ROWS, :]
-            nc.sync.dma_start(out=rows.rearrange("(c s) d -> c s d", s=PACK), in_=out_sb[:])
+            out_sb = staging.tile([P, 2, 2 * D], F32, name="out_sb")
+            nc.scalar.copy(
+                out=out_sb[:].rearrange("p x e -> p (x e)"),
+                in_=accs[(i, chunk)][:].rearrange("p u d -> p (u d)"),
+            )
+            rows = out[b, h, chunk * ROWS : (chunk + 1) * ROWS, :].rearrange(
+                "(x c a e) d -> a c x (e d)", x=2, a=2, e=2
+            )
+            for a in range(2):
+                nc.sync.dma_start(out=rows[a], in_=out_sb[a * HALF : (a + 1) * HALF, :, :])
 
         gamma_bf = const.tile([P, H], BF16)
         nc.sync.dma_start(out=gamma_bf[:], in_=gamma.partition_broadcast(P))
@@ -200,28 +304,87 @@ def tile_multiscaleretention_pa_kernel(tc, q, k, v, gamma, out):
 
         ln_gamma = const.tile([P, H], F32)
         nc.scalar.activation(out=ln_gamma[:], in_=gamma_bf[:], func=ACT.Ln)
-        nc.vector.tensor_scalar_min(out=ln_gamma[:], in0=ln_gamma[:], scalar1=-1e-25)
 
         identity = const.tile([P, P], BF16)
         make_identity(nc, identity[:])
-        steps = const.tile([P, SPAN], I32)
-        nc.gpsimd.iota(steps[:], pattern=[[1, SPAN]], base=-REACH, channel_multiplier=-PACK)
-        behind = const.tile([P, SPAN], F32)
-        nc.vector.tensor_scalar(
-            out=behind[:], in0=steps[:], scalar1=0.0, scalar2=FAR, op0=ALU.is_lt, op1=ALU.mult
+        lead = const.tile([P, WIDTH], F32)
+        nc.gpsimd.iota(
+            lead[:],
+            pattern=[[1, WIDTH]],
+            base=0,
+            channel_multiplier=-PACK,
+            allow_small_or_imprecise_dtypes=True,
         )
-        distance = const.tile([P, SPAN], F32)
-        nc.vector.scalar_tensor_tensor(
-            out=distance[:], in0=steps[:], scalar=0.0, in1=behind[:], op0=ALU.max, op1=ALU.add
+        extra = const.tile([P, 2, 2], F32)
+        nc.gpsimd.iota(
+            extra[:],
+            pattern=[[ROWS // 2, 2], [1, 2]],
+            base=0,
+            channel_multiplier=0,
+            allow_small_or_imprecise_dtypes=True,
         )
 
-        decay_table(0)
-        transpose(0, 0)
-        copy_transposed(0, 0)
-        transpose(0, 1)
-        copy_transposed(0, 1)
+        distance = const.tile([P, TABLE], F32)
+        behind = const.tile([P, WIDTH], F32)
+        near, far = 1 - PACK, ROWS // 2 + 1 - PACK
+
+        def distances(kind, p0, p1, offset):
+            at = (PACKED, LATE0, LATE1).index(kind) * WIDTH
+            nc.vector.tensor_scalar(
+                out=behind[p0:p1, :],
+                in0=lead[p0:p1, :],
+                scalar1=float(-offset),
+                scalar2=FAR,
+                op0=ALU.is_lt,
+                op1=ALU.mult,
+            )
+            nc.vector.scalar_tensor_tensor(
+                out=distance[p0:p1, at : at + WIDTH],
+                in0=lead[p0:p1, :],
+                scalar=float(offset),
+                in1=behind[p0:p1, :],
+                op0=ALU.add,
+                op1=ALU.max,
+            )
+
+        distances(PACKED, 0, HALF, near)
+        distances(PACKED, HALF, P, far)
+        nc.vector.tensor_scalar_min(out=ln_gamma[:], in0=ln_gamma[:], scalar1=-1e-25)
+        distances(LATE0, 0, P, far)
+        distances(LATE1, 0, HALF, near)
+        distances(LATE1, HALF, P, far + ROWS // 2)
+        for a in range(2):
+            at = PAST_AT + a * STRIP
+            nc.vector.tensor_scalar_add(
+                out=distance[:, at : at + STRIP],
+                in0=lead[:, 0:STRIP],
+                scalar1=float(ROWS + 1 - PACK + 2 * a),
+            )
+        farther = const.tile([P, H, 4], F32)
+        nc.vector.tensor_tensor(
+            out=farther[:],
+            in0=ln_gamma[:].unsqueeze(2).to_broadcast([P, H, 4]),
+            in1=extra[:].rearrange("p x e -> p (x e)").unsqueeze(1).to_broadcast([P, H, 4]),
+            op=ALU.mult,
+        )
+        padded_k = [const.tile([P, PACK, 4, HALF], BF16, name="padded_k%d" % n) for n in range(2)]
+        padded_v = [
+            const.tile([P, CHUNKS * D], U32, name="padded_v%d" % n, align_bytes=64) for n in range(2)
+        ]
+        for n in range(2):
+            nc.gpsimd.memset(padded_k[n][:], 0.0)
+            nc.gpsimd.memset(padded_v[n][:], 0)
+
+        transpose_k(0)
+        transpose_q(0)
+        decay_table(0, 0, 2 * WIDTH)
+        copy_k_padded(0)
+        copy_k(0)
+        copy_q(0)
         for n in range(V_BANKS):
             fill_v(n)
+        decay_table(0, 2 * WIDTH, TABLE)
+        nc.scalar.activation(out=farther[:], in_=farther[:], func=ACT.Exp)
         for n in range(G_BANKS):
             fill_g(n)
             drain_g(n)
@@ -238,43 +401,40 @@ def tile_multiscaleretention_pa_kernel(tc, q, k, v, gamma, out):
                 fill_v(v0 + x + V_BANKS)
 
             if nxt:
-                transpose(i + 1, 0)
-                copy_transposed(i + 1, 0)
+                transpose_k(i + 1)
+                copy_k_padded(i + 1)
+                copy_k(i + 1)
             if i > 0:
                 retention(i - 1, 1)
             for j in range(NG):
                 mask_g(g0 + j)
-                if j == 0:
-                    fill_g(g0 + 2)
-                    drain_g(g0 + 2)
             step(0)
             step(1)
             step(2)
             if nxt:
-                transpose(i + 1, 1)
-                copy_transposed(i + 1, 1)
-            step(3)
-            step(4)
-            step(5)
-            fill_g(g0 + NG)
-            fill_g(g0 + NG + 1)
-            step(6)
-            step(7)
-            step(8)
+                transpose_q(i + 1)
+                copy_q(i + 1)
+                if (i + 1) % B == 0:
+                    decay_table((i + 1) // B, 0, TABLE)
             if i > 0:
                 store(i - 1, 0)
                 store(i - 1, 1)
+            step(3)
+            step(4)
             if nxt:
                 regroup_v(i + 1)
-                if (i + 1) % B == 0:
-                    decay_table((i + 1) // B)
-            drain_g(g0 + NG)
-            drain_g(g0 + NG + 1)
+            for j in range(NG):
+                fill_g(g0 + NG + j)
+                drain_g(g0 + NG + j)
+            step(5)
+            step(6)
+            step(7)
             quantise_v(i)
-            quantise(i, DIAG0)
-            quantise(i, PAST)
+            quantise(i, "early")
+            pad_v(i)
             retention(i, 0)
-            quantise(i, DIAG1)
+            quantise(i, "past")
+            quantise(i, "late")
         retention(HEADS - 1, 1)
         store(HEADS - 1, 0)
         store(HEADS - 1, 1)

@@ -45,6 +45,7 @@ def tile_multiscaleretention_pa_kernel(tc, q, k, v, gamma, out):
         tables = ctx.enter_context(tc.tile_pool(name="tables", bufs=2))
         loads = ctx.enter_context(tc.tile_pool(name="loads", bufs=3))
         operands = ctx.enter_context(tc.tile_pool(name="operands", bufs=2))
+        keys_pool = ctx.enter_context(tc.tile_pool(name="keys", bufs=3))
         quantised = ctx.enter_context(tc.tile_pool(name="quantised", bufs=2))
         staging = ctx.enter_context(tc.tile_pool(name="staging", bufs=3))
         transposed_psum = ctx.enter_context(tc.psum_pool(name="transposed_psum", bufs=1))
@@ -114,12 +115,12 @@ def tile_multiscaleretention_pa_kernel(tc, q, k, v, gamma, out):
             turned_q[i] = ps
 
         def copy_k(i):
-            sb = operands.tile([P, PACK, CHUNKS * 2, HALF], BF16, name="kT")
+            sb = keys_pool.tile([P, PACK, CHUNKS * 2, HALF], BF16, name="kT")
             nc.scalar.copy(out=sb[:], in_=turned_k[i][:])
             kT[i] = sb
 
         def copy_k_padded(i):
-            nc.scalar.copy(out=padded_k[i % 2][:, :, ::3, :], in_=turned_k[i][:, :, ::3, :])
+            nc.scalar.copy(out=padded_k[i % 3][:, :, ::3, :], in_=turned_k[i][:, :, ::3, :])
 
         def copy_q(i):
             sb = operands.tile([P, CHUNKS, 2, 2, P], BF16, name="qT")
@@ -163,8 +164,8 @@ def tile_multiscaleretention_pa_kernel(tc, q, k, v, gamma, out):
                 t = PACK - 1 - w
                 if kind == PACKED:
                     terms = [
-                        (keys(padded_k[i % 2], t, 0), queries(0, 0)),
-                        (keys(padded_k[i % 2], t, 2), queries(1, 0)),
+                        (keys(padded_k[i % 3], t, 0), queries(0, 0)),
+                        (keys(padded_k[i % 3], t, 2), queries(1, 0)),
                     ]
                 elif kind == LATE0:
                     terms = [(keys(kT[i], t, 0), queries(0, 1))]
@@ -301,6 +302,7 @@ def tile_multiscaleretention_pa_kernel(tc, q, k, v, gamma, out):
         nc.sync.dma_start(out=gamma_bf[:], in_=gamma.partition_broadcast(P))
         load(0)
         load(1)
+        load(2)
 
         ln_gamma = const.tile([P, H], F32)
         nc.scalar.activation(out=ln_gamma[:], in_=gamma_bf[:], func=ACT.Ln)
@@ -367,13 +369,14 @@ def tile_multiscaleretention_pa_kernel(tc, q, k, v, gamma, out):
             in1=extra[:].rearrange("p x e -> p (x e)").unsqueeze(1).to_broadcast([P, H, 4]),
             op=ALU.mult,
         )
-        padded_k = [const.tile([P, PACK, 4, HALF], BF16, name="padded_k%d" % n) for n in range(2)]
+        padded_k = [const.tile([P, PACK, 4, HALF], BF16, name="padded_k%d" % n) for n in range(3)]
         padded_v = [
             const.tile([P, CHUNKS * D], U32, name="padded_v%d" % n, align_bytes=64) for n in range(2)
         ]
-        for n in range(2):
-            nc.gpsimd.memset(padded_k[n][:], 0.0)
-            nc.gpsimd.memset(padded_v[n][:], 0)
+        for tile in padded_k:
+            nc.gpsimd.memset(tile[:], 0.0)
+        for tile in padded_v:
+            nc.gpsimd.memset(tile[:], 0)
 
         transpose_k(0)
         transpose_q(0)
@@ -385,56 +388,56 @@ def tile_multiscaleretention_pa_kernel(tc, q, k, v, gamma, out):
             fill_v(n)
         decay_table(0, 2 * WIDTH, TABLE)
         nc.scalar.activation(out=farther[:], in_=farther[:], func=ACT.Exp)
-        for n in range(G_BANKS):
+        for n in range(NG):
             fill_g(n)
             drain_g(n)
+        transpose_k(1)
+        copy_k_padded(1)
+        copy_k(1)
+        transpose_q(1)
         regroup_v(0)
 
         for i in range(HEADS):
-            nxt = i + 1 < HEADS
-            if i + 2 < HEADS:
-                load(i + 2)
+            nxt, nxt2 = i + 1 < HEADS, i + 2 < HEADS
+            if i + 3 < HEADS:
+                load(i + 3)
             v0, g0 = i * NV, i * NG
 
             def step(x):
                 mask_v(v0 + x)
                 fill_v(v0 + x + V_BANKS)
 
-            if nxt:
-                transpose_k(i + 1)
-                copy_k_padded(i + 1)
-                copy_k(i + 1)
-            if i > 0:
-                retention(i - 1, 1)
             for j in range(NG):
                 mask_g(g0 + j)
+            if nxt:
+                copy_q(i + 1)
+            if i > 0:
+                retention(i - 1, 1)
+                store(i - 1, 1)
             step(0)
             step(1)
             step(2)
             if nxt:
-                transpose_q(i + 1)
-                copy_q(i + 1)
                 if (i + 1) % B == 0:
                     decay_table((i + 1) // B, 0, TABLE)
-            if i > 0:
-                store(i - 1, 0)
-                store(i - 1, 1)
-            step(3)
-            step(4)
-            if nxt:
                 regroup_v(i + 1)
+            if nxt2:
+                transpose_k(i + 2)
+                copy_k_padded(i + 2)
+                copy_k(i + 2)
+            for x in range(3, NV):
+                step(x)
             for j in range(NG):
                 fill_g(g0 + NG + j)
                 drain_g(g0 + NG + j)
-            step(5)
-            step(6)
-            step(7)
+            if nxt2:
+                transpose_q(i + 2)
             quantise_v(i)
             quantise(i, "early")
             pad_v(i)
             retention(i, 0)
+            store(i, 0)
             quantise(i, "past")
             quantise(i, "late")
         retention(HEADS - 1, 1)
-        store(HEADS - 1, 0)
         store(HEADS - 1, 1)

@@ -23,16 +23,19 @@ TILES = S // P
 UNIT = P * PACK
 STRIP = UNIT // 2
 
-PACKED, LATE0, PAST, LATE1 = 0, 1, 2, 3
-V_UNITS = [(kind, x, e) for kind, x in ((PACKED, 0), (LATE0, 0), (PAST, 0), (PAST, 1)) for e in range(2)]
-G_UNITS = [(LATE1, 0, e) for e in range(2)]
+EARLY, LATE, PAST = 0, 1, 2
+V_UNITS = [(EARLY, 0), (EARLY, 1), (EARLY, 2), (EARLY, 3), (LATE, 0), (LATE, 1), (PAST, 0), (PAST, 1)]
+G_UNITS = [(PAST, 2), (PAST, 3)]
 NV, NG = len(V_UNITS), len(G_UNITS)
 V_BANKS, G_BANKS = 3, 2
 
 WIDTH = STRIP + PACK
-PAST_AT = 3 * WIDTH
-TABLE = PAST_AT + UNIT
+ROWS_OF_TABLE = 4
+PAST_AT = ROWS_OF_TABLE * WIDTH
+TABLE = PAST_AT + UNIT + PACK
 FAR = 1e30
+
+V_AT = 12 * HALF
 
 FLOPS = B * H * 2 * 2 * D * (512 * 512 + 512 * 1024)
 
@@ -54,7 +57,7 @@ def tile_multiscaleretention_pa_kernel(tc, q, k, v, gamma, out):
         out_psum = ctx.enter_context(tc.psum_pool(name="out_psum", bufs=1))
         ctx.enter_context(tc.manual_schedule())
 
-        raw, turned_k, turned_q, kT, qT, v_mx, decay = {}, {}, {}, {}, {}, {}, {}
+        raw, turned_k, turned_q, kT, qT, decay = {}, {}, {}, {}, {}, {}
         v_bank, g_bank, staged, accs, grouped, score_mx = {}, {}, {}, {}, {}, {}
 
         def load_keys(i, name, src):
@@ -123,64 +126,64 @@ def tile_multiscaleretention_pa_kernel(tc, q, k, v, gamma, out):
             nc.scalar.copy(out=padded_k[i % 3][:, :, ::3, :], in_=turned_k[i][:, :, ::3, :])
 
         def copy_q(i):
-            sb = operands.tile([P, CHUNKS, 2, 2, P], BF16, name="qT")
+            sb = operands.tile([P, CHUNKS, PACK, P], BF16, name="qT")
             copy = nc.vector.tensor_copy if i == 0 else nc.scalar.copy
             copy(
-                out=sb[:].rearrange("p g a e c -> p (g a e c)"),
+                out=sb[:].rearrange("p g s c -> p (g s c)"),
                 in_=turned_q[i][:].rearrange("p j c -> p (j c)"),
             )
             qT[i] = sb
 
+        def group_tile(i, name):
+            if (i, name) not in grouped:
+                slots = 16 if name == "near" else 8
+                grouped[(i, name)] = quantised.tile(
+                    [P, slots, STRIP], BF16, name="grouped_" + name, align_bytes=64
+                )
+            return grouped[(i, name)]
+
         def regroup_v(i):
-            t = operands.tile([P, CHUNKS * D * PACK], BF16, name="v_grouped", align_bytes=64)
             nc.scalar.copy(
-                out=t[:].rearrange("p (g d w) -> p g d w", g=CHUNKS, w=PACK),
+                out=group_tile(i, "near")[:, 12:16, :]
+                .rearrange("p k e -> p (k e)")
+                .rearrange("p (g d w) -> p g d w", g=CHUNKS, w=PACK),
                 in_=raw[i][2][:].rearrange("p g t d -> p g d t")[:, :, :, ::-1],
             )
-            v_mx[i] = t
-
-        def quantise_v(i):
-            codes = quantised.tile([P, CHUNKS * D], U32, name="v_codes", align_bytes=64)
-            scales = quantised.tile([P, CHUNKS * D], U8, name="v_scales", align_bytes=64)
-            nc.vector.quantize_mx(out=codes[:].bitcast(FP8X4), scales=scales[:], in_=v_mx[i][:])
-            v_mx[i] = (codes, scales)
 
         def pad_v(i):
-            codes = v_mx[i][0]
+            codes = score_mx[(i, "near")][0]
             for g, p0 in ((0, 0), (1, HALF)):
-                nc.vector.tensor_copy(
-                    out=padded_v[i % 2][p0 : p0 + HALF, g * D : (g + 1) * D].bitcast(I32),
-                    in_=codes[p0 : p0 + HALF, g * D : (g + 1) * D].bitcast(I32),
+                at = V_AT + g * D
+                nc.gpsimd.tensor_copy(
+                    out=padded_v[i % 2][p0 : p0 + HALF, g * D : (g + 1) * D],
+                    in_=codes[p0 : p0 + HALF, at : at + D],
                 )
 
-        def fill(bank, i, kind, x, e):
-            def queries(chunk, half):
-                return qT[i][:, chunk, :, e, half * HALF : (half + 1) * HALF]
+        def fill(bank, i, kind, s):
+            def queries(chunk, first, count, c0, c1):
+                return qT[i][:, chunk, first : first + count, c0:c1]
 
             def keys(tile, t, first):
                 return tile[:, t, first : first + 2, :].rearrange("p b c -> p (b c)")
 
             for w in range(PACK):
                 t = PACK - 1 - w
-                if kind == PACKED:
+                if kind == EARLY:
                     terms = [
-                        (keys(padded_k[i % 3], t, 0), queries(0, 0)),
-                        (keys(padded_k[i % 3], t, 2), queries(1, 0)),
+                        (0, 1, keys(padded_k[i % 3], t, 0), queries(0, s, 1, 0, HALF), True, False),
+                        (0, 1, keys(padded_k[i % 3], t, 2), queries(1, s, 1, 0, HALF), False, True),
+                        (1, 2, keys(kT[i], t, 0), queries(0, s, 1, HALF, P), True, True),
                     ]
-                elif kind == LATE0:
-                    terms = [(keys(kT[i], t, 0), queries(0, 1))]
-                elif kind == LATE1:
-                    terms = [(keys(kT[i], t, 2), queries(1, 1))]
+                elif kind == LATE:
+                    terms = [(0, 2, keys(kT[i], t, 2), queries(1, 2 * s, 2, HALF, P), True, True)]
                 else:
-                    terms = [(keys(kT[i], t, 0), queries(1, x))]
-                for n, (lhsT, rhs) in enumerate(terms):
-                    nc.tensor.matmul(
-                        bank[:, w, :, :],
-                        lhsT=lhsT,
-                        rhs=rhs,
-                        start=(n == 0),
-                        stop=(n == len(terms) - 1),
-                    )
+                    terms = [(0, 2, keys(kT[i], t, 0), queries(1, s, 1, 0, P), True, True)]
+                for b0, b1, lhsT, rhs, start, stop in terms:
+                    dst = bank[:, w, b0:b1, :]
+                    if kind != LATE:
+                        dst = dst.rearrange("p b c -> p (b c)")
+                        rhs = rhs.rearrange("p s c -> p (s c)")
+                    nc.tensor.matmul(dst, lhsT=lhsT, rhs=rhs, start=start, stop=stop)
 
         def fill_v(n):
             if n < HEADS * NV:
@@ -192,105 +195,92 @@ def tile_multiscaleretention_pa_kernel(tc, q, k, v, gamma, out):
                 g_bank[n] = g_psum.tile([P, PACK, 2, HALF], F32, name="g_scores")
                 fill(g_bank[n], n // NG, *G_UNITS[n % NG])
 
-        def strip(i, kind, a, e):
-            first = (PACKED, LATE0, LATE1).index(kind) * WIDTH + 2 * a + e
-            return decay[i // B][:, first : first + STRIP]
-
-        def masked(i, kind, x, e):
-            name = "late" if kind == LATE1 else "past" if kind == PAST else "early"
-            units = 2 if kind == LATE1 else 4
-            if (i, name) not in grouped:
-                grouped[(i, name)] = quantised.tile(
-                    [P, units, 2, STRIP], BF16, name="grouped_" + name, align_bytes=64
+        def weights(i, kind, s):
+            table = decay[i // B]
+            if kind == PAST:
+                return table[:, PAST_AT + s : PAST_AT + s + UNIT].rearrange(
+                    "p (b e) -> p b e", b=2
                 )
-            return grouped[(i, name)][:, 2 * (1 if kind == LATE0 else x) + e, :, :]
+            row, first = (0, s) if kind == EARLY else (2, 2 * s)
+            return table[:, 0:PAST_AT].rearrange("p (r j) -> p r j", r=ROWS_OF_TABLE)[
+                :, row : row + 2, first : first + STRIP
+            ]
+
+        def masked(i, kind, s):
+            if kind == LATE:
+                return group_tile(i, "near")[:, 8 + s : 12 : 2, :]
+            slot = 2 * (s % 2) + s // 2
+            if kind == EARLY:
+                return group_tile(i, "near")[:, slot : 8 : 4, :]
+            return group_tile(i, "past")[:, slot : 8 : 4, :]
 
         def mask_v(n):
             i = n // NV
-            kind, x, e = V_UNITS[n % NV]
-            dst = masked(i, kind, x, e)
-            if kind == PAST:
-                nc.vector.scalar_tensor_tensor(
-                    out=dst.rearrange("p a (c w) -> p a c w", w=PACK),
-                    in0=v_bank[n][:].rearrange("p w a c -> p a c w"),
-                    scalar=farther[:, i // B, 2 * x + e : 2 * x + e + 1],
-                    in1=decay[i // B][:, PAST_AT:TABLE].rearrange(
-                        "p (a c w) -> p a c w", a=2, w=PACK
-                    ),
-                    op0=ALU.mult,
-                    op1=ALU.mult,
-                )
-            else:
-                for a in range(2):
-                    nc.vector.tensor_tensor(
-                        out=dst[:, a, :].rearrange("p (c w) -> p c w", w=PACK),
-                        in0=v_bank[n][:, :, a, :].rearrange("p w c -> p c w"),
-                        in1=strip(i, kind, a, e).rearrange("p (c w) -> p c w", w=PACK),
-                        op=ALU.mult,
-                    )
+            unit = V_UNITS[n % NV]
+            nc.vector.tensor_tensor(
+                out=masked(i, *unit).rearrange("p b (c w) -> p b c w", w=PACK),
+                in0=v_bank[n][:].rearrange("p w b c -> p b c w"),
+                in1=weights(i, *unit).rearrange("p b (c w) -> p b c w", w=PACK),
+                op=ALU.mult,
+            )
 
         def drain_g(n):
             if n < HEADS * NG:
                 staged[n] = staging.tile([P, 2, STRIP], F32, name="staged")
                 nc.scalar.copy(
-                    out=staged[n][:].rearrange("p a (c w) -> p a c w", w=PACK),
-                    in_=g_bank[n][:].rearrange("p w a c -> p a c w"),
+                    out=staged[n][:].rearrange("p b (c w) -> p b c w", w=PACK),
+                    in_=g_bank[n][:].rearrange("p w b c -> p b c w"),
                 )
 
         def mask_g(n):
             i = n // NG
-            kind, x, e = G_UNITS[n % NG]
-            dst = masked(i, kind, x, e)
-            for a in range(2):
-                nc.gpsimd.tensor_tensor(
-                    out=dst[:, a, :],
-                    in0=staged[n][:, a, :],
-                    in1=strip(i, kind, a, e),
-                    op=ALU.mult,
-                )
+            unit = G_UNITS[n % NG]
+            nc.gpsimd.tensor_tensor(
+                out=masked(i, *unit), in0=staged[n][:], in1=weights(i, *unit), op=ALU.mult
+            )
 
         def quantise(i, name):
-            units = 2 if name == "late" else 4
-            codes = quantised.tile([P, units * P], U32, name="codes_" + name, align_bytes=64)
-            scales = quantised.tile([P, units * P], U8, name="scales_" + name, align_bytes=64)
+            words = 16 * HALF if name == "near" else 8 * HALF
+            codes = quantised.tile([P, words], U32, name="codes_" + name, align_bytes=64)
+            scales = quantised.tile([P, words], U8, name="scales_" + name, align_bytes=64)
             nc.vector.quantize_mx(
                 out=codes[:].bitcast(FP8X4),
                 scales=scales[:],
-                in_=grouped[(i, name)][:].rearrange("p u a e -> p (u a e)"),
+                in_=grouped[(i, name)][:].rearrange("p k e -> p (k e)"),
             )
             score_mx[(i, name)] = (codes, scales)
 
-        def retention(i, chunk):
-            v_codes, v_scales = v_mx[i]
-            acc = out_psum.tile([P, PACK, D], F32, name="acc%d" % chunk)
-            for x in range(2):
+        def retention(i, x):
+            near, past = score_mx[(i, "near")], score_mx[(i, "past")]
+            if x == 1:
+                accs[i] = [
+                    out_psum.tile([P, PACK, D], F32, name="acc%d" % chunk) for chunk in range(CHUNKS)
+                ]
+            for chunk in range(CHUNKS):
                 for e in range(2):
-                    slot = 2 * x + e
-                    if chunk == 0:
-                        passes = [("early", slot, padded_v[i % 2] if x == 0 else v_codes, 0)]
-                    elif x == 0:
-                        passes = [("past", slot, v_codes, 0), ("early", e, padded_v[i % 2], 1)]
+                    passes = [] if chunk == 0 else [(past, 2 * x + e, near[0], V_AT, 0)]
+                    if x == 0:
+                        passes.append((near, e, padded_v[i % 2], chunk * D, chunk))
                     else:
-                        passes = [("past", slot, v_codes, 0), ("late", e, v_codes, 1)]
-                    for n, (name, unit, values, g) in enumerate(passes):
-                        codes, scales = score_mx[(i, name)]
+                        unit = 2 + e if chunk == 0 else 4 + e
+                        passes.append((near, unit, near[0], V_AT + chunk * D, chunk))
+                    for n, ((codes, scales), unit, values, at, g) in enumerate(passes):
                         nc.tensor.matmul_mx(
-                            out=acc[:, slot, :],
+                            out=accs[i][chunk][:, 2 * x + e, :],
                             lhsT=codes[:, unit * P : (unit + 1) * P].bitcast(FP8X4),
                             lhsT_scale=scales[:, unit * P : (unit + 1) * P],
-                            rhs=values[:, g * D : (g + 1) * D].bitcast(FP8X4),
-                            rhs_scale=v_scales[:, g * D : (g + 1) * D],
+                            rhs=values[:, at : at + D].bitcast(FP8X4),
+                            rhs_scale=near[1][:, V_AT + g * D : V_AT + (g + 1) * D],
                             start=(n == 0),
                             stop=(n == len(passes) - 1),
                         )
-            accs[(i, chunk)] = acc
 
         def store(i, chunk):
             h, b = divmod(i, B)
             out_sb = staging.tile([P, 2, 2 * D], F32, name="out_sb")
             nc.scalar.copy(
                 out=out_sb[:].rearrange("p x e -> p (x e)"),
-                in_=accs[(i, chunk)][:].rearrange("p u d -> p (u d)"),
+                in_=accs[i][chunk][:].rearrange("p u d -> p (u d)"),
             )
             rows = out[b, h, chunk * ROWS : (chunk + 1) * ROWS, :].rearrange(
                 "(x c a e) d -> a c x (e d)", x=2, a=2, e=2
@@ -309,20 +299,12 @@ def tile_multiscaleretention_pa_kernel(tc, q, k, v, gamma, out):
 
         identity = const.tile([P, P], BF16)
         make_identity(nc, identity[:])
-        lead = const.tile([P, WIDTH], F32)
+        lead = const.tile([P, UNIT + PACK], F32)
         nc.gpsimd.iota(
             lead[:],
-            pattern=[[1, WIDTH]],
+            pattern=[[1, UNIT + PACK]],
             base=0,
             channel_multiplier=-PACK,
-            allow_small_or_imprecise_dtypes=True,
-        )
-        extra = const.tile([P, 2, 2], F32)
-        nc.gpsimd.iota(
-            extra[:],
-            pattern=[[ROWS // 2, 2], [1, 2]],
-            base=0,
-            channel_multiplier=0,
             allow_small_or_imprecise_dtypes=True,
         )
 
@@ -330,44 +312,33 @@ def tile_multiscaleretention_pa_kernel(tc, q, k, v, gamma, out):
         behind = const.tile([P, WIDTH], F32)
         near, far = 1 - PACK, ROWS // 2 + 1 - PACK
 
-        def distances(kind, p0, p1, offset):
-            at = (PACKED, LATE0, LATE1).index(kind) * WIDTH
+        def distances(row, p0, p1, offset):
             nc.vector.tensor_scalar(
                 out=behind[p0:p1, :],
-                in0=lead[p0:p1, :],
+                in0=lead[p0:p1, 0:WIDTH],
                 scalar1=float(-offset),
                 scalar2=FAR,
                 op0=ALU.is_lt,
                 op1=ALU.mult,
             )
             nc.vector.scalar_tensor_tensor(
-                out=distance[p0:p1, at : at + WIDTH],
-                in0=lead[p0:p1, :],
+                out=distance[p0:p1, row * WIDTH : (row + 1) * WIDTH],
+                in0=lead[p0:p1, 0:WIDTH],
                 scalar=float(offset),
                 in1=behind[p0:p1, :],
                 op0=ALU.add,
                 op1=ALU.max,
             )
 
-        distances(PACKED, 0, HALF, near)
-        distances(PACKED, HALF, P, far)
+        distances(0, 0, HALF, near)
+        distances(0, HALF, P, far)
         nc.vector.tensor_scalar_min(out=ln_gamma[:], in0=ln_gamma[:], scalar1=-1e-25)
-        distances(LATE0, 0, P, far)
-        distances(LATE1, 0, HALF, near)
-        distances(LATE1, HALF, P, far + ROWS // 2)
-        for a in range(2):
-            at = PAST_AT + a * STRIP
-            nc.vector.tensor_scalar_add(
-                out=distance[:, at : at + STRIP],
-                in0=lead[:, 0:STRIP],
-                scalar1=float(ROWS + 1 - PACK + 2 * a),
-            )
-        farther = const.tile([P, H, 4], F32)
-        nc.vector.tensor_tensor(
-            out=farther[:],
-            in0=ln_gamma[:].unsqueeze(2).to_broadcast([P, H, 4]),
-            in1=extra[:].rearrange("p x e -> p (x e)").unsqueeze(1).to_broadcast([P, H, 4]),
-            op=ALU.mult,
+        distances(1, 0, P, far)
+        for row in (2, 3):
+            distances(row, 0, HALF, near + row - 2)
+            distances(row, HALF, P, far + ROWS // 2 + row - 2)
+        nc.vector.tensor_scalar_add(
+            out=distance[:, PAST_AT:TABLE], in0=lead[:], scalar1=float(ROWS + 1 - PACK)
         )
         padded_k = [const.tile([P, PACK, 4, HALF], BF16, name="padded_k%d" % n) for n in range(3)]
         padded_v = [
@@ -387,7 +358,6 @@ def tile_multiscaleretention_pa_kernel(tc, q, k, v, gamma, out):
         for n in range(V_BANKS):
             fill_v(n)
         decay_table(0, 2 * WIDTH, TABLE)
-        nc.scalar.activation(out=farther[:], in_=farther[:], func=ACT.Exp)
         for n in range(NG):
             fill_g(n)
             drain_g(n)
@@ -395,6 +365,7 @@ def tile_multiscaleretention_pa_kernel(tc, q, k, v, gamma, out):
         copy_k_padded(1)
         copy_k(1)
         transpose_q(1)
+        copy_q(1)
         regroup_v(0)
 
         for i in range(HEADS):
@@ -407,37 +378,43 @@ def tile_multiscaleretention_pa_kernel(tc, q, k, v, gamma, out):
                 mask_v(v0 + x)
                 fill_v(v0 + x + V_BANKS)
 
+            if i > 0:
+                pad_v(i - 1)
             for j in range(NG):
                 mask_g(g0 + j)
             if nxt:
-                copy_q(i + 1)
+                regroup_v(i + 1)
+            h = i // B + 1
+            if h < H:
+                if i % B == 0:
+                    decay_table(h, 0, PAST_AT)
+                else:
+                    decay_table(h, PAST_AT, TABLE)
             if i > 0:
                 retention(i - 1, 1)
-                store(i - 1, 1)
             step(0)
-            step(1)
-            step(2)
-            if nxt:
-                if (i + 1) % B == 0:
-                    decay_table((i + 1) // B, 0, TABLE)
-                regroup_v(i + 1)
             if nxt2:
                 transpose_k(i + 2)
                 copy_k_padded(i + 2)
                 copy_k(i + 2)
+            step(1)
+            step(2)
+            if i > 0:
+                retention(i - 1, 0)
+                store(i - 1, 0)
+                store(i - 1, 1)
             for x in range(3, NV):
                 step(x)
+            if nxt2:
+                transpose_q(i + 2)
+                copy_q(i + 2)
             for j in range(NG):
                 fill_g(g0 + NG + j)
                 drain_g(g0 + NG + j)
-            if nxt2:
-                transpose_q(i + 2)
-            quantise_v(i)
-            quantise(i, "early")
-            pad_v(i)
-            retention(i, 0)
-            store(i, 0)
+            quantise(i, "near")
             quantise(i, "past")
-            quantise(i, "late")
+        pad_v(HEADS - 1)
         retention(HEADS - 1, 1)
+        retention(HEADS - 1, 0)
+        store(HEADS - 1, 0)
         store(HEADS - 1, 1)

@@ -24,8 +24,8 @@ UNIT = P * PACK
 STRIP = UNIT // 2
 
 EARLY, LATE, PAST = 0, 1, 2
-V_UNITS = [(EARLY, 0), (EARLY, 1), (EARLY, 2), (EARLY, 3), (LATE, 0), (LATE, 1), (PAST, 0), (PAST, 1)]
-G_UNITS = [(PAST, 2), (PAST, 3)]
+V_UNITS = [(EARLY, 0), (EARLY, 1), (EARLY, 2), (EARLY, 3), (LATE, 0), (LATE, 1), (PAST, 0), (PAST, 2)]
+G_UNITS = [(PAST, 1), (PAST, 3)]
 NV, NG = len(V_UNITS), len(G_UNITS)
 V_BANKS, G_BANKS = 3, 2
 
@@ -33,6 +33,7 @@ WIDTH = STRIP + PACK
 ROWS_OF_TABLE = 4
 PAST_AT = ROWS_OF_TABLE * WIDTH
 TABLE = PAST_AT + UNIT + PACK
+WARM_UPS = 18
 FAR = 1e30
 
 V_AT = 12 * HALF
@@ -75,6 +76,22 @@ def tile_multiscaleretention_pa_kernel(tc, q, k, v, gamma, out):
                     ),
                 )
             return t
+
+        def turn_k(i):
+            if i < HEADS:
+                transpose_k(i)
+                copy_k_padded(i)
+                copy_k(i)
+
+        def prepare(i):
+            if i + 1 < HEADS:
+                regroup_v(i + 1)
+            h = i // B + 1
+            if h < H:
+                if i % B == 0:
+                    decay_table(h, 0, PAST_AT)
+                else:
+                    decay_table(h, PAST_AT, TABLE)
 
         def load(i):
             h, b = divmod(i, B)
@@ -119,7 +136,11 @@ def tile_multiscaleretention_pa_kernel(tc, q, k, v, gamma, out):
 
         def copy_k(i):
             sb = keys_pool.tile([P, PACK, CHUNKS * 2, HALF], BF16, name="kT")
-            nc.scalar.copy(out=sb[:], in_=turned_k[i][:])
+            copy = nc.vector.tensor_copy if i == 0 else nc.scalar.copy
+            copy(
+                out=sb[:].rearrange("p t b c -> p (t b c)"),
+                in_=turned_k[i][:].rearrange("p t b c -> p (t b c)"),
+            )
             kT[i] = sb
 
         def copy_k_padded(i):
@@ -127,7 +148,7 @@ def tile_multiscaleretention_pa_kernel(tc, q, k, v, gamma, out):
 
         def copy_q(i):
             sb = operands.tile([P, CHUNKS, PACK, P], BF16, name="qT")
-            copy = nc.vector.tensor_copy if i == 0 else nc.scalar.copy
+            copy = nc.vector.tensor_copy if i < 2 else nc.scalar.copy
             copy(
                 out=sb[:].rearrange("p g s c -> p (g s c)"),
                 in_=turned_q[i][:].rearrange("p j c -> p (j c)"),
@@ -143,7 +164,8 @@ def tile_multiscaleretention_pa_kernel(tc, q, k, v, gamma, out):
             return grouped[(i, name)]
 
         def regroup_v(i):
-            nc.scalar.copy(
+            copy = nc.vector.tensor_copy if i == 0 else nc.scalar.copy
+            copy(
                 out=group_tile(i, "near")[:, 12:16, :]
                 .rearrange("p k e -> p (k e)")
                 .rearrange("p (g d w) -> p g d w", g=CHUNKS, w=PACK),
@@ -152,11 +174,12 @@ def tile_multiscaleretention_pa_kernel(tc, q, k, v, gamma, out):
 
         def pad_v(i):
             codes = score_mx[(i, "near")][0]
+            engine, dtype = (nc.gpsimd, U32) if i < HEADS - 1 else (nc.vector, I32)
             for g, p0 in ((0, 0), (1, HALF)):
                 at = V_AT + g * D
-                nc.gpsimd.tensor_copy(
-                    out=padded_v[i % 2][p0 : p0 + HALF, g * D : (g + 1) * D],
-                    in_=codes[p0 : p0 + HALF, at : at + D],
+                engine.tensor_copy(
+                    out=padded_v[i % 2][p0 : p0 + HALF, g * D : (g + 1) * D].bitcast(dtype),
+                    in_=codes[p0 : p0 + HALF, at : at + D].bitcast(dtype),
                 )
 
         def fill(bank, i, kind, s):
@@ -209,10 +232,10 @@ def tile_multiscaleretention_pa_kernel(tc, q, k, v, gamma, out):
         def masked(i, kind, s):
             if kind == LATE:
                 return group_tile(i, "near")[:, 8 + s : 12 : 2, :]
-            slot = 2 * (s % 2) + s // 2
+            e, a = s % 2, s // 2
             if kind == EARLY:
-                return group_tile(i, "near")[:, slot : 8 : 4, :]
-            return group_tile(i, "past")[:, slot : 8 : 4, :]
+                return group_tile(i, "near")[:, 2 * e + a : 8 : 4, :]
+            return group_tile(i, "past")[:, 4 * e + a : 4 * e + a + 3 : 2, :]
 
         def mask_v(n):
             i = n // NV
@@ -250,15 +273,15 @@ def tile_multiscaleretention_pa_kernel(tc, q, k, v, gamma, out):
             )
             score_mx[(i, name)] = (codes, scales)
 
-        def retention(i, x):
-            near, past = score_mx[(i, "near")], score_mx[(i, "past")]
-            if x == 1:
+        def retention(i, x, chunks=range(CHUNKS)):
+            near, past = score_mx[(i, "near")], score_mx.get((i, "past"))
+            if i not in accs:
                 accs[i] = [
                     out_psum.tile([P, PACK, D], F32, name="acc%d" % chunk) for chunk in range(CHUNKS)
                 ]
-            for chunk in range(CHUNKS):
+            for chunk in chunks:
                 for e in range(2):
-                    passes = [] if chunk == 0 else [(past, 2 * x + e, near[0], V_AT, 0)]
+                    passes = [] if chunk == 0 else [(past, 2 * e + x, near[0], V_AT, 0)]
                     if x == 0:
                         passes.append((near, e, padded_v[i % 2], chunk * D, chunk))
                     else:
@@ -278,7 +301,8 @@ def tile_multiscaleretention_pa_kernel(tc, q, k, v, gamma, out):
         def store(i, chunk):
             h, b = divmod(i, B)
             out_sb = staging.tile([P, 2, 2 * D], F32, name="out_sb")
-            nc.scalar.copy(
+            copy = nc.vector.tensor_copy if (i, chunk) == (HEADS - 1, 0) else nc.scalar.copy
+            copy(
                 out=out_sb[:].rearrange("p x e -> p (x e)"),
                 in_=accs[i][chunk][:].rearrange("p u d -> p (u d)"),
             )
@@ -289,7 +313,7 @@ def tile_multiscaleretention_pa_kernel(tc, q, k, v, gamma, out):
                 nc.sync.dma_start(out=rows[a], in_=out_sb[a * HALF : (a + 1) * HALF, :, :])
 
         gamma_bf = const.tile([P, H], BF16)
-        nc.sync.dma_start(out=gamma_bf[:], in_=gamma.partition_broadcast(P))
+        nc.scalar.dma_start(out=gamma_bf[:], in_=gamma.partition_broadcast(P))
         load(0)
         load(1)
         load(2)
@@ -297,46 +321,61 @@ def tile_multiscaleretention_pa_kernel(tc, q, k, v, gamma, out):
         ln_gamma = const.tile([P, H], F32)
         nc.scalar.activation(out=ln_gamma[:], in_=gamma_bf[:], func=ACT.Ln)
 
+        zeros = const.tile([P, P], BF16)
+        nc.vector.memset(zeros[:], 0.0)
+        idle = out_psum.tile([P, PACK, P], F32, name="acc0")
+        for n in range(WARM_UPS):
+            nc.tensor.matmul(
+                idle[:, n % PACK, :], lhsT=zeros[:], rhs=zeros[:], start=True, stop=True
+            )
+
         identity = const.tile([P, P], BF16)
         make_identity(nc, identity[:])
         lead = const.tile([P, UNIT + PACK], F32)
-        nc.gpsimd.iota(
-            lead[:],
-            pattern=[[1, UNIT + PACK]],
-            base=0,
-            channel_multiplier=-PACK,
-            allow_small_or_imprecise_dtypes=True,
-        )
+        for first, last in ((0, WIDTH), (WIDTH, UNIT + PACK)):
+            nc.gpsimd.iota(
+                lead[:, first:last],
+                pattern=[[1, last - first]],
+                base=first,
+                channel_multiplier=-PACK,
+                allow_small_or_imprecise_dtypes=True,
+            )
+
+        near, far = 1 - PACK, ROWS // 2 + 1 - PACK
+        offset = [const.tile([P, 2, 2], F32, name="offset%d" % n) for n in range(2)]
+        for row, (low, high) in enumerate(
+            ((near, far), (far, far), (near, far + ROWS // 2), (near + 1, far + ROWS // 2 + 1))
+        ):
+            for p0, value in ((0, low), (HALF, high)):
+                engine = nc.vector if row < 2 else nc.gpsimd
+                engine.memset(offset[row // 2][p0 : p0 + HALF, row % 2, 0:1], float(value))
+                engine.memset(offset[row // 2][p0 : p0 + HALF, row % 2, 1:2], float(-value))
 
         distance = const.tile([P, TABLE], F32)
-        behind = const.tile([P, WIDTH], F32)
-        near, far = 1 - PACK, ROWS // 2 + 1 - PACK
+        behind = const.tile([P, ROWS_OF_TABLE, WIDTH], F32)
 
-        def distances(row, p0, p1, offset):
-            nc.vector.tensor_scalar(
-                out=behind[p0:p1, :],
-                in0=lead[p0:p1, 0:WIDTH],
-                scalar1=float(-offset),
-                scalar2=FAR,
-                op0=ALU.is_lt,
-                op1=ALU.mult,
-            )
-            nc.vector.scalar_tensor_tensor(
-                out=distance[p0:p1, row * WIDTH : (row + 1) * WIDTH],
-                in0=lead[p0:p1, 0:WIDTH],
-                scalar=float(offset),
-                in1=behind[p0:p1, :],
-                op0=ALU.add,
-                op1=ALU.max,
-            )
+        def distances(rows):
+            for row in rows:
+                nc.vector.tensor_scalar(
+                    out=behind[:, row, :],
+                    in0=lead[:, 0:WIDTH],
+                    scalar1=offset[row // 2][:, row % 2, 1:2],
+                    scalar2=FAR,
+                    op0=ALU.is_lt,
+                    op1=ALU.mult,
+                )
+            for row in rows:
+                nc.vector.scalar_tensor_tensor(
+                    out=distance[:, row * WIDTH : (row + 1) * WIDTH],
+                    in0=lead[:, 0:WIDTH],
+                    scalar=offset[row // 2][:, row % 2, 0:1],
+                    in1=behind[:, row, :],
+                    op0=ALU.add,
+                    op1=ALU.max,
+                )
 
-        distances(0, 0, HALF, near)
-        distances(0, HALF, P, far)
         nc.vector.tensor_scalar_min(out=ln_gamma[:], in0=ln_gamma[:], scalar1=-1e-25)
-        distances(1, 0, P, far)
-        for row in (2, 3):
-            distances(row, 0, HALF, near + row - 2)
-            distances(row, HALF, P, far + ROWS // 2 + row - 2)
+        distances((0, 1))
         nc.vector.tensor_scalar_add(
             out=distance[:, PAST_AT:TABLE], in0=lead[:], scalar1=float(ROWS + 1 - PACK)
         )
@@ -351,25 +390,23 @@ def tile_multiscaleretention_pa_kernel(tc, q, k, v, gamma, out):
 
         transpose_k(0)
         transpose_q(0)
-        decay_table(0, 0, 2 * WIDTH)
         copy_k_padded(0)
+        decay_table(0, 0, 2 * WIDTH)
         copy_k(0)
         copy_q(0)
+        distances((2, 3))
+        regroup_v(0)
+        decay_table(0, PAST_AT, TABLE)
+        turn_k(1)
         for n in range(V_BANKS):
             fill_v(n)
-        decay_table(0, 2 * WIDTH, TABLE)
+        decay_table(0, 2 * WIDTH, PAST_AT)
+        transpose_q(1)
         for n in range(NG):
             fill_g(n)
             drain_g(n)
-        transpose_k(1)
-        copy_k_padded(1)
-        copy_k(1)
-        transpose_q(1)
-        copy_q(1)
-        regroup_v(0)
 
         for i in range(HEADS):
-            nxt, nxt2 = i + 1 < HEADS, i + 2 < HEADS
             if i + 3 < HEADS:
                 load(i + 3)
             v0, g0 = i * NV, i * NG
@@ -382,39 +419,43 @@ def tile_multiscaleretention_pa_kernel(tc, q, k, v, gamma, out):
                 pad_v(i - 1)
             for j in range(NG):
                 mask_g(g0 + j)
-            if nxt:
-                regroup_v(i + 1)
-            h = i // B + 1
-            if h < H:
-                if i % B == 0:
-                    decay_table(h, 0, PAST_AT)
-                else:
-                    decay_table(h, PAST_AT, TABLE)
             if i > 0:
+                prepare(i)
                 retention(i - 1, 1)
-            step(0)
-            if nxt2:
-                transpose_k(i + 2)
-                copy_k_padded(i + 2)
-                copy_k(i + 2)
-            step(1)
-            step(2)
+                step(0)
+                turn_k(i + 2)
+                step(1)
+                step(2)
+            else:
+                step(0)
+                step(1)
+                copy_q(1)
+                step(2)
+                step(3)
+                turn_k(2)
+                prepare(0)
             if i > 0:
                 retention(i - 1, 0)
                 store(i - 1, 0)
                 store(i - 1, 1)
-            for x in range(3, NV):
+            for x in range(3 if i > 0 else 4, NV):
                 step(x)
-            if nxt2:
+            if i + 2 < HEADS:
                 transpose_q(i + 2)
                 copy_q(i + 2)
             for j in range(NG):
                 fill_g(g0 + NG + j)
                 drain_g(g0 + NG + j)
             quantise(i, "near")
-            quantise(i, "past")
-        pad_v(HEADS - 1)
-        retention(HEADS - 1, 1)
-        retention(HEADS - 1, 0)
-        store(HEADS - 1, 0)
-        store(HEADS - 1, 1)
+            if i < HEADS - 1:
+                quantise(i, "past")
+
+        i = HEADS - 1
+        pad_v(i)
+        quantise(i, "past")
+        retention(i, 1, (0,))
+        retention(i, 0, (0,))
+        retention(i, 1, (1,))
+        retention(i, 0, (1,))
+        store(i, 0)
+        store(i, 1)

@@ -24,8 +24,8 @@ UNIT = P * PACK
 STRIP = UNIT // 2
 
 EARLY, LATE, PAST = 0, 1, 2
-V_UNITS = [(EARLY, 0), (EARLY, 1), (EARLY, 2), (EARLY, 3), (LATE, 0), (LATE, 1), (PAST, 0), (PAST, 2)]
-G_UNITS = [(PAST, 1), (PAST, 3)]
+V_UNITS = [(PAST, 0), (EARLY, 0), (EARLY, 1), (EARLY, 2), (EARLY, 3), (LATE, 0), (LATE, 1)]
+G_UNITS = [(PAST, 1), (PAST, 3), (PAST, 2)]
 NV, NG = len(V_UNITS), len(G_UNITS)
 V_BANKS, G_BANKS = 3, 2
 
@@ -33,7 +33,7 @@ WIDTH = STRIP + PACK
 ROWS_OF_TABLE = 4
 PAST_AT = ROWS_OF_TABLE * WIDTH
 TABLE = PAST_AT + UNIT + PACK
-WARM_UPS = 18
+WARM_UPS = 12
 FAR = 1e30
 
 V_AT = 12 * HALF
@@ -83,13 +83,18 @@ def tile_multiscaleretention_pa_kernel(tc, q, k, v, gamma, out):
                 copy_k_padded(i)
                 copy_k(i)
 
-        def prepare(i):
-            if i + 1 < HEADS:
-                regroup_v(i + 1)
+        def shifted_row(h):
+            nc.sync.dma_start(
+                out=decay[h][:, 3 * WIDTH : 4 * WIDTH - 1],
+                in_=decay[h][:, 2 * WIDTH + 1 : 3 * WIDTH],
+            )
+
+        def next_table(i):
             h = i // B + 1
             if h < H:
                 if i % B == 0:
-                    decay_table(h, 0, PAST_AT)
+                    decay_table(h, 0, 3 * WIDTH)
+                    shifted_row(h)
                 else:
                     decay_table(h, PAST_AT, TABLE)
 
@@ -104,7 +109,7 @@ def tile_multiscaleretention_pa_kernel(tc, q, k, v, gamma, out):
             raw[i] = (k_sb, q_sb, v_sb)
 
         def decay_table(h, first, last):
-            if first == 0:
+            if h not in decay:
                 decay[h] = tables.tile([P, TABLE], F32, name="table")
             nc.scalar.activation(
                 out=decay[h][:, first:last],
@@ -165,21 +170,23 @@ def tile_multiscaleretention_pa_kernel(tc, q, k, v, gamma, out):
 
         def regroup_v(i):
             copy = nc.vector.tensor_copy if i == 0 else nc.scalar.copy
-            copy(
-                out=group_tile(i, "near")[:, 12:16, :]
-                .rearrange("p k e -> p (k e)")
-                .rearrange("p (g d w) -> p g d w", g=CHUNKS, w=PACK),
-                in_=raw[i][2][:].rearrange("p g t d -> p g d t")[:, :, :, ::-1],
-            )
+            dst = group_tile(i, "near")[:, 12:16, :].rearrange("p k e -> p (k e)")
+            for g in range(CHUNKS):
+                copy(
+                    out=dst[:, g * D * PACK : (g + 1) * D * PACK].rearrange(
+                        "p (b c w) -> p b w c", c=4, w=PACK
+                    ),
+                    in_=raw[i][2][:, g, ::-1, :].rearrange("p w (b c) -> p b w c", c=4),
+                )
 
         def pad_v(i):
             codes = score_mx[(i, "near")][0]
-            engine, dtype = (nc.gpsimd, U32) if i < HEADS - 1 else (nc.vector, I32)
+            copy = nc.sync.dma_start if i < HEADS - 1 else nc.vector.tensor_copy
             for g, p0 in ((0, 0), (1, HALF)):
                 at = V_AT + g * D
-                engine.tensor_copy(
-                    out=padded_v[i % 2][p0 : p0 + HALF, g * D : (g + 1) * D].bitcast(dtype),
-                    in_=codes[p0 : p0 + HALF, at : at + D].bitcast(dtype),
+                copy(
+                    out=padded_v[i % 2][p0 : p0 + HALF, g * D : (g + 1) * D].bitcast(I32),
+                    in_=codes[p0 : p0 + HALF, at : at + D].bitcast(I32),
                 )
 
         def fill(bank, i, kind, s):
@@ -343,9 +350,7 @@ def tile_multiscaleretention_pa_kernel(tc, q, k, v, gamma, out):
 
         near, far = 1 - PACK, ROWS // 2 + 1 - PACK
         offset = [const.tile([P, 2, 2], F32, name="offset%d" % n) for n in range(2)]
-        for row, (low, high) in enumerate(
-            ((near, far), (far, far), (near, far + ROWS // 2), (near + 1, far + ROWS // 2 + 1))
-        ):
+        for row, (low, high) in enumerate(((near, far), (far, far), (near, far + ROWS // 2))):
             for p0, value in ((0, low), (HALF, high)):
                 engine = nc.vector if row < 2 else nc.gpsimd
                 engine.memset(offset[row // 2][p0 : p0 + HALF, row % 2, 0:1], float(value))
@@ -375,10 +380,10 @@ def tile_multiscaleretention_pa_kernel(tc, q, k, v, gamma, out):
                 )
 
         nc.vector.tensor_scalar_min(out=ln_gamma[:], in0=ln_gamma[:], scalar1=-1e-25)
-        distances((0, 1))
         nc.vector.tensor_scalar_add(
             out=distance[:, PAST_AT:TABLE], in0=lead[:], scalar1=float(ROWS + 1 - PACK)
         )
+        distances((0, 1, 2))
         padded_k = [const.tile([P, PACK, 4, HALF], BF16, name="padded_k%d" % n) for n in range(3)]
         padded_v = [
             const.tile([P, CHUNKS * D], U32, name="padded_v%d" % n, align_bytes=64) for n in range(2)
@@ -390,19 +395,19 @@ def tile_multiscaleretention_pa_kernel(tc, q, k, v, gamma, out):
 
         transpose_k(0)
         transpose_q(0)
+        decay_table(0, PAST_AT, TABLE)
         copy_k_padded(0)
         decay_table(0, 0, 2 * WIDTH)
         copy_k(0)
         copy_q(0)
-        distances((2, 3))
         regroup_v(0)
-        decay_table(0, PAST_AT, TABLE)
         turn_k(1)
         for n in range(V_BANKS):
             fill_v(n)
-        decay_table(0, 2 * WIDTH, PAST_AT)
+        decay_table(0, 2 * WIDTH, 3 * WIDTH)
+        shifted_row(0)
         transpose_q(1)
-        for n in range(NG):
+        for n in range(2):
             fill_g(n)
             drain_g(n)
 
@@ -415,39 +420,40 @@ def tile_multiscaleretention_pa_kernel(tc, q, k, v, gamma, out):
                 mask_v(v0 + x)
                 fill_v(v0 + x + V_BANKS)
 
-            if i > 0:
-                pad_v(i - 1)
-            for j in range(NG):
+            for j in range(min(NG, 2)):
                 mask_g(g0 + j)
             if i > 0:
-                prepare(i)
+                if i + 1 < HEADS:
+                    regroup_v(i + 1)
                 retention(i - 1, 1)
-                step(0)
-                turn_k(i + 2)
-                step(1)
-                step(2)
-            else:
-                step(0)
-                step(1)
-                copy_q(1)
-                step(2)
-                step(3)
-                turn_k(2)
-                prepare(0)
-            if i > 0:
-                retention(i - 1, 0)
-                store(i - 1, 0)
-                store(i - 1, 1)
-            for x in range(3 if i > 0 else 4, NV):
+            for x in range(NV):
+                if i == 0 and x == 2:
+                    copy_q(1)
                 step(x)
-            if i + 2 < HEADS:
-                transpose_q(i + 2)
-                copy_q(i + 2)
-            for j in range(NG):
-                fill_g(g0 + NG + j)
-                drain_g(g0 + NG + j)
+                if x == (1 if i > 0 else 3):
+                    turn_k(i + 2)
+                    if i == 0:
+                        regroup_v(1)
+                        next_table(0)
+                if x == 0:
+                    fill_g(g0 + 2)
+                    drain_g(g0 + 2)
+                    mask_g(g0 + 2)
+                    if i > 0:
+                        next_table(i)
+                if x == 3 and i > 0:
+                    retention(i - 1, 0)
+                    store(i - 1, 0)
+                    store(i - 1, 1)
+                if x == 5 and i + 2 < HEADS:
+                    transpose_q(i + 2)
+                    copy_q(i + 2)
+            for n in range(g0 + NG, g0 + NG + 2):
+                fill_g(n)
+                drain_g(n)
             quantise(i, "near")
             if i < HEADS - 1:
+                pad_v(i)
                 quantise(i, "past")
 
         i = HEADS - 1

@@ -23,9 +23,9 @@ TILES = S // P
 UNIT = P * PACK
 STRIP = UNIT // 2
 
-EARLY, LATE, PAST = 0, 1, 2
-V_UNITS = [(PAST, 0), (EARLY, 0), (EARLY, 1), (EARLY, 2), (EARLY, 3), (LATE, 0), (LATE, 1)]
-G_UNITS = [(PAST, 1), (PAST, 3), (PAST, 2)]
+EARLY, LATE, PAST, PAST_LO, PAST_HI = 0, 1, 2, 3, 4
+V_UNITS = [(PAST, 0), (EARLY, 0), (EARLY, 1), (EARLY, 2), (EARLY, 3), (LATE, 0), (LATE, 1), (PAST_LO, 2)]
+G_UNITS = [(PAST, 1), (PAST, 3), (PAST_HI, 2)]
 NV, NG = len(V_UNITS), len(G_UNITS)
 V_BANKS, G_BANKS = 3, 2
 
@@ -170,14 +170,12 @@ def tile_multiscaleretention_pa_kernel(tc, q, k, v, gamma, out):
 
         def regroup_v(i):
             copy = nc.vector.tensor_copy if i == 0 else nc.scalar.copy
-            dst = group_tile(i, "near")[:, 12:16, :].rearrange("p k e -> p (k e)")
-            for g in range(CHUNKS):
-                copy(
-                    out=dst[:, g * D * PACK : (g + 1) * D * PACK].rearrange(
-                        "p (b c w) -> p b w c", c=4, w=PACK
-                    ),
-                    in_=raw[i][2][:, g, ::-1, :].rearrange("p w (b c) -> p b w c", c=4),
-                )
+            copy(
+                out=group_tile(i, "near")[:, 12:16, :]
+                .rearrange("p k e -> p (k e)")
+                .rearrange("p (g d w) -> p g d w", g=CHUNKS, w=PACK),
+                in_=raw[i][2][:].rearrange("p g t d -> p g d t")[:, :, :, ::-1],
+            )
 
         def pad_v(i):
             codes = score_mx[(i, "near")][0]
@@ -188,6 +186,9 @@ def tile_multiscaleretention_pa_kernel(tc, q, k, v, gamma, out):
                     out=padded_v[i % 2][p0 : p0 + HALF, g * D : (g + 1) * D].bitcast(I32),
                     in_=codes[p0 : p0 + HALF, at : at + D].bitcast(I32),
                 )
+
+        def strips(kind):
+            return slice(1 if kind == PAST_HI else 0, 1 if kind == PAST_LO else 2)
 
         def fill(bank, i, kind, s):
             def queries(chunk, first, count, c0, c1):
@@ -207,7 +208,9 @@ def tile_multiscaleretention_pa_kernel(tc, q, k, v, gamma, out):
                 elif kind == LATE:
                     terms = [(0, 2, keys(kT[i], t, 2), queries(1, 2 * s, 2, HALF, P), True, True)]
                 else:
-                    terms = [(0, 2, keys(kT[i], t, 0), queries(1, s, 1, 0, P), True, True)]
+                    b = strips(kind)
+                    part = queries(1, s, 1, b.start * HALF, b.stop * HALF)
+                    terms = [(b.start, b.stop, keys(kT[i], t, 0), part, True, True)]
                 for b0, b1, lhsT, rhs, start, stop in terms:
                     dst = bank[:, w, b0:b1, :]
                     if kind != LATE:
@@ -227,10 +230,10 @@ def tile_multiscaleretention_pa_kernel(tc, q, k, v, gamma, out):
 
         def weights(i, kind, s):
             table = decay[i // B]
-            if kind == PAST:
+            if kind >= PAST:
                 return table[:, PAST_AT + s : PAST_AT + s + UNIT].rearrange(
                     "p (b e) -> p b e", b=2
-                )
+                )[:, strips(kind), :]
             row, first = (0, s) if kind == EARLY else (2, 2 * s)
             return table[:, 0:PAST_AT].rearrange("p (r j) -> p r j", r=ROWS_OF_TABLE)[
                 :, row : row + 2, first : first + STRIP
@@ -242,14 +245,14 @@ def tile_multiscaleretention_pa_kernel(tc, q, k, v, gamma, out):
             e, a = s % 2, s // 2
             if kind == EARLY:
                 return group_tile(i, "near")[:, 2 * e + a : 8 : 4, :]
-            return group_tile(i, "past")[:, 4 * e + a : 4 * e + a + 3 : 2, :]
+            return group_tile(i, "past")[:, 4 * e + a : 4 * e + a + 3 : 2, :][:, strips(kind), :]
 
         def mask_v(n):
             i = n // NV
             unit = V_UNITS[n % NV]
             nc.vector.tensor_tensor(
                 out=masked(i, *unit).rearrange("p b (c w) -> p b c w", w=PACK),
-                in0=v_bank[n][:].rearrange("p w b c -> p b c w"),
+                in0=v_bank[n][:, :, strips(unit[0]), :].rearrange("p w b c -> p b c w"),
                 in1=weights(i, *unit).rearrange("p b (c w) -> p b c w", w=PACK),
                 op=ALU.mult,
             )
@@ -257,16 +260,20 @@ def tile_multiscaleretention_pa_kernel(tc, q, k, v, gamma, out):
         def drain_g(n):
             if n < HEADS * NG:
                 staged[n] = staging.tile([P, 2, STRIP], F32, name="staged")
+                b = strips(G_UNITS[n % NG][0])
                 nc.scalar.copy(
-                    out=staged[n][:].rearrange("p b (c w) -> p b c w", w=PACK),
-                    in_=g_bank[n][:].rearrange("p w b c -> p b c w"),
+                    out=staged[n][:, b, :].rearrange("p b (c w) -> p b c w", w=PACK),
+                    in_=g_bank[n][:, :, b, :].rearrange("p w b c -> p b c w"),
                 )
 
         def mask_g(n):
             i = n // NG
             unit = G_UNITS[n % NG]
             nc.gpsimd.tensor_tensor(
-                out=masked(i, *unit), in0=staged[n][:], in1=weights(i, *unit), op=ALU.mult
+                out=masked(i, *unit),
+                in0=staged[n][:, strips(unit[0]), :],
+                in1=weights(i, *unit),
+                op=ALU.mult,
             )
 
         def quantise(i, name):
@@ -406,10 +413,10 @@ def tile_multiscaleretention_pa_kernel(tc, q, k, v, gamma, out):
             fill_v(n)
         decay_table(0, 2 * WIDTH, 3 * WIDTH)
         shifted_row(0)
-        transpose_q(1)
         for n in range(2):
             fill_g(n)
             drain_g(n)
+        transpose_q(1)
 
         for i in range(HEADS):
             if i + 3 < HEADS:
@@ -427,10 +434,10 @@ def tile_multiscaleretention_pa_kernel(tc, q, k, v, gamma, out):
                     regroup_v(i + 1)
                 retention(i - 1, 1)
             for x in range(NV):
-                if i == 0 and x == 2:
+                if i == 0 and x == 3:
                     copy_q(1)
                 step(x)
-                if x == (1 if i > 0 else 3):
+                if x == (2 if i > 0 else 3):
                     turn_k(i + 2)
                     if i == 0:
                         regroup_v(1)
@@ -441,11 +448,11 @@ def tile_multiscaleretention_pa_kernel(tc, q, k, v, gamma, out):
                     mask_g(g0 + 2)
                     if i > 0:
                         next_table(i)
-                if x == 3 and i > 0:
+                if x == 4 and i > 0:
                     retention(i - 1, 0)
                     store(i - 1, 0)
                     store(i - 1, 1)
-                if x == 5 and i + 2 < HEADS:
+                if x == 6 and i + 2 < HEADS:
                     transpose_q(i + 2)
                     copy_q(i + 2)
             for n in range(g0 + NG, g0 + NG + 2):

from contextlib import ExitStack

import concourse.mybir as mybir
from concourse.masks import make_identity

BF16 = mybir.dt.bfloat16
F32 = mybir.dt.float32
I32 = mybir.dt.int32
U32 = mybir.dt.uint32
U8 = mybir.dt.uint8
FP8X4 = mybir.dt.float8_e4m3fn_x4
ALU = mybir.AluOpType
ACT = mybir.ActivationFunctionType

B, H, S, D = 2, 8, 1024, 128
HEADS = B * H
P = 128
HALF = P // 2
PACK = 4
ROWS = P * PACK
CHUNKS = S // ROWS
TILES = S // P
UNIT = P * PACK
STRIP = UNIT // 2

EARLY, LATE, PAST, PAST_LO, PAST_HI = 0, 1, 2, 3, 4
V_UNITS = [(PAST, 0), (EARLY, 0), (EARLY, 1), (EARLY, 2), (EARLY, 3), (LATE, 0), (LATE, 1), (PAST_LO, 2)]
G_UNITS = [(PAST, 1), (PAST, 3), (PAST_HI, 2)]
NV, NG = len(V_UNITS), len(G_UNITS)
V_BANKS, G_BANKS = 3, 2

WIDTH = STRIP + PACK
ROWS_OF_TABLE = 4
PAST_AT = ROWS_OF_TABLE * WIDTH
TABLE = PAST_AT + UNIT + PACK
WARM_UPS = 12
FAR = 1e30

V_AT = 12 * HALF

FLOPS = B * H * 2 * 2 * D * (512 * 512 + 512 * 1024)


def tile_multiscaleretention_pa_kernel(tc, q, k, v, gamma, out):
    nc = tc.nc

    with ExitStack() as ctx:
        const = ctx.enter_context(tc.tile_pool(name="const", bufs=1))
        tables = ctx.enter_context(tc.tile_pool(name="tables", bufs=2))
        loads = ctx.enter_context(tc.tile_pool(name="loads", bufs=3))
        operands = ctx.enter_context(tc.tile_pool(name="operands", bufs=2))
        keys_pool = ctx.enter_context(tc.tile_pool(name="keys", bufs=3))
        quantised = ctx.enter_context(tc.tile_pool(name="quantised", bufs=2))
        staging = ctx.enter_context(tc.tile_pool(name="staging", bufs=3))
        transposed_psum = ctx.enter_context(tc.psum_pool(name="transposed_psum", bufs=1))
        v_psum = ctx.enter_context(tc.psum_pool(name="v_psum", bufs=V_BANKS))
        g_psum = ctx.enter_context(tc.psum_pool(name="g_psum", bufs=G_BANKS))
        out_psum = ctx.enter_context(tc.psum_pool(name="out_psum", bufs=1))
        ctx.enter_context(tc.manual_schedule())

        raw, turned_k, turned_q, kT, qT, decay = {}, {}, {}, {}, {}, {}
        v_bank, g_bank, staged, accs, grouped, score_mx = {}, {}, {}, {}, {}, {}

        def load_keys(i, name, src):
            h, b = divmod(i, B)
            t = loads.tile([P, CHUNKS, PACK, D], BF16, name="raw_" + name)
            for p0, p1, g, first in (
                (0, P, 0, 0),
                (0, HALF, 1, ROWS + ROWS // 2),
                (HALF, P, 1, ROWS),
            ):
                nc.sync.dma_start(
                    out=t[p0:p1, g, :, :],
                    in_=src[b, h, first : first + PACK * (p1 - p0), :].rearrange(
                        "(p t) d -> p t d", t=PACK
                    ),
                )
            return t

        def turn_k(i):
            if i < HEADS:
                transpose_k(i)
                copy_k_padded(i)
                copy_k(i)

        def shifted_row(h):
            nc.sync.dma_start(
                out=decay[h][:, 3 * WIDTH : 4 * WIDTH - 1],
                in_=decay[h][:, 2 * WIDTH + 1 : 3 * WIDTH],
            )

        def next_table(i):
            h = i // B + 1
            if h < H:
                if i % B == 0:
                    decay_table(h, 0, 3 * WIDTH)
                    shifted_row(h)
                else:
                    decay_table(h, PAST_AT, TABLE)

        def load(i):
            h, b = divmod(i, B)
            k_sb = load_keys(i, "k", k)
            q_sb = loads.tile([P, CHUNKS, PACK, D], BF16, name="raw_q")
            nc.sync.dma_start(
                out=q_sb[:], in_=q[b, h].rearrange("(g p t) d -> p g t d", p=P, t=PACK)
            )
            v_sb = load_keys(i, "v", v)
            raw[i] = (k_sb, q_sb, v_sb)

        def decay_table(h, first, last):
            if h not in decay:
                decay[h] = tables.tile([P, TABLE], F32, name="table")
            nc.scalar.activation(
                out=decay[h][:, first:last],
                in_=distance[:, first:last],
                func=ACT.Exp,
                scale=ln_gamma[:, h : h + 1],
            )

        def transpose_k(i):
            ps = transposed_psum.tile([P, PACK, CHUNKS * 2, HALF], BF16, name="turned")
            for t in range(PACK):
                for g in range(CHUNKS):
                    nc.tensor.transpose(
                        ps[:, t, 2 * g : 2 * g + 2, :].rearrange("p b c -> p (b c)"),
                        raw[i][0][:, g, t, :],
                        identity[:],
                    )
            turned_k[i] = ps

        def transpose_q(i):
            if i == 0:
                ps = out_psum.tile([P, TILES, P], BF16, name="acc1")
            else:
                ps = transposed_psum.tile([P, TILES, P], BF16, name="turned")
            for j in range(TILES):
                g, s = divmod(j, PACK)
                nc.tensor.transpose(ps[:, j, :], raw[i][1][:, g, s, :], identity[:])
            turned_q[i] = ps

        def copy_k(i):
            sb = keys_pool.tile([P, PACK, CHUNKS * 2, HALF], BF16, name="kT")
            copy = nc.vector.tensor_copy if i == 0 else nc.scalar.copy
            copy(
                out=sb[:].rearrange("p t b c -> p (t b c)"),
                in_=turned_k[i][:].rearrange("p t b c -> p (t b c)"),
            )
            kT[i] = sb

        def copy_k_padded(i):
            nc.scalar.copy(out=padded_k[i % 3][:, :, ::3, :], in_=turned_k[i][:, :, ::3, :])

        def copy_q(i):
            sb = operands.tile([P, CHUNKS, PACK, P], BF16, name="qT")
            copy = nc.vector.tensor_copy if i < 2 else nc.scalar.copy
            copy(
                out=sb[:].rearrange("p g s c -> p (g s c)"),
                in_=turned_q[i][:].rearrange("p j c -> p (j c)"),
            )
            qT[i] = sb

        def group_tile(i, name):
            if (i, name) not in grouped:
                slots = 16 if name == "near" else 8
                grouped[(i, name)] = quantised.tile(
                    [P, slots, STRIP], BF16, name="grouped_" + name, align_bytes=64
                )
            return grouped[(i, name)]

        def regroup_v(i):
            copy = nc.vector.tensor_copy if i == 0 else nc.scalar.copy
            copy(
                out=group_tile(i, "near")[:, 12:16, :]
                .rearrange("p k e -> p (k e)")
                .rearrange("p (g d w) -> p g d w", g=CHUNKS, w=PACK),
                in_=raw[i][2][:].rearrange("p g t d -> p g d t")[:, :, :, ::-1],
            )

        def pad_v(i):
            codes = score_mx[(i, "near")][0]
            copy = nc.sync.dma_start if i < HEADS - 1 else nc.vector.tensor_copy
            for g, p0 in ((0, 0), (1, HALF)):
                at = V_AT + g * D
                copy(
                    out=padded_v[i % 2][p0 : p0 + HALF, g * D : (g + 1) * D].bitcast(I32),
                    in_=codes[p0 : p0 + HALF, at : at + D].bitcast(I32),
                )

        def strips(kind):
            return slice(1 if kind == PAST_HI else 0, 1 if kind == PAST_LO else 2)

        def fill(bank, i, kind, s):
            def queries(chunk, first, count, c0, c1):
                return qT[i][:, chunk, first : first + count, c0:c1]

            def keys(tile, t, first):
                return tile[:, t, first : first + 2, :].rearrange("p b c -> p (b c)")

            for w in range(PACK):
                t = PACK - 1 - w
                if kind == EARLY:
                    terms = [
                        (0, 1, keys(padded_k[i % 3], t, 0), queries(0, s, 1, 0, HALF), True, False),
                        (0, 1, keys(padded_k[i % 3], t, 2), queries(1, s, 1, 0, HALF), False, True),
                        (1, 2, keys(kT[i], t, 0), queries(0, s, 1, HALF, P), True, True),
                    ]
                elif kind == LATE:
                    terms = [(0, 2, keys(kT[i], t, 2), queries(1, 2 * s, 2, HALF, P), True, True)]
                else:
                    b = strips(kind)
                    part = queries(1, s, 1, b.start * HALF, b.stop * HALF)
                    terms = [(b.start, b.stop, keys(kT[i], t, 0), part, True, True)]
                for b0, b1, lhsT, rhs, start, stop in terms:
                    dst = bank[:, w, b0:b1, :]
                    if kind != LATE:
                        dst = dst.rearrange("p b c -> p (b c)")
                        rhs = rhs.rearrange("p s c -> p (s c)")
                    nc.tensor.matmul(dst, lhsT=lhsT, rhs=rhs, start=start, stop=stop)

        def fill_v(n):
            if n < HEADS * NV:
                v_bank[n] = v_psum.tile([P, PACK, 2, HALF], F32, name="v_scores")
                fill(v_bank[n], n // NV, *V_UNITS[n % NV])

        def fill_g(n):
            if n < HEADS * NG:
                g_bank[n] = g_psum.tile([P, PACK, 2, HALF], F32, name="g_scores")
                fill(g_bank[n], n // NG, *G_UNITS[n % NG])

        def weights(i, kind, s):
            table = decay[i // B]
            if kind >= PAST:
                return table[:, PAST_AT + s : PAST_AT + s + UNIT].rearrange(
                    "p (b e) -> p b e", b=2
                )[:, strips(kind), :]
            row, first = (0, s) if kind == EARLY else (2, 2 * s)
            return table[:, 0:PAST_AT].rearrange("p (r j) -> p r j", r=ROWS_OF_TABLE)[
                :, row : row + 2, first : first + STRIP
            ]

        def masked(i, kind, s):
            if kind == LATE:
                return group_tile(i, "near")[:, 8 + s : 12 : 2, :]
            e, a = s % 2, s // 2
            if kind == EARLY:
                return group_tile(i, "near")[:, 2 * e + a : 8 : 4, :]
            return group_tile(i, "past")[:, 4 * e + a : 4 * e + a + 3 : 2, :][:, strips(kind), :]

        def mask_v(n):
            i = n // NV
            unit = V_UNITS[n % NV]
            nc.vector.tensor_tensor(
                out=masked(i, *unit).rearrange("p b (c w) -> p b c w", w=PACK),
                in0=v_bank[n][:, :, strips(unit[0]), :].rearrange("p w b c -> p b c w"),
                in1=weights(i, *unit).rearrange("p b (c w) -> p b c w", w=PACK),
                op=ALU.mult,
            )

        def drain_g(n):
            if n < HEADS * NG:
                staged[n] = staging.tile([P, 2, STRIP], F32, name="staged")
                b = strips(G_UNITS[n % NG][0])
                nc.scalar.copy(
                    out=staged[n][:, b, :].rearrange("p b (c w) -> p b c w", w=PACK),
                    in_=g_bank[n][:, :, b, :].rearrange("p w b c -> p b c w"),
                )

        def mask_g(n):
            i = n // NG
            unit = G_UNITS[n % NG]
            nc.gpsimd.tensor_tensor(
                out=masked(i, *unit),
                in0=staged[n][:, strips(unit[0]), :],
                in1=weights(i, *unit),
                op=ALU.mult,
            )

        def quantise(i, name):
            words = 16 * HALF if name == "near" else 8 * HALF
            codes = quantised.tile([P, words], U32, name="codes_" + name, align_bytes=64)
            scales = quantised.tile([P, words], U8, name="scales_" + name, align_bytes=64)
            nc.vector.quantize_mx(
                out=codes[:].bitcast(FP8X4),
                scales=scales[:],
                in_=grouped[(i, name)][:].rearrange("p k e -> p (k e)"),
            )
            score_mx[(i, name)] = (codes, scales)

        def retention(i, x, chunks=range(CHUNKS)):
            near, past = score_mx[(i, "near")], score_mx.get((i, "past"))
            if i not in accs:
                accs[i] = [
                    out_psum.tile([P, PACK, D], F32, name="acc%d" % chunk) for chunk in range(CHUNKS)
                ]
            for chunk in chunks:
                for e in range(2):
                    passes = [] if chunk == 0 else [(past, 2 * e + x, near[0], V_AT, 0)]
                    if x == 0:
                        passes.append((near, e, padded_v[i % 2], chunk * D, chunk))
                    else:
                        unit = 2 + e if chunk == 0 else 4 + e
                        passes.append((near, unit, near[0], V_AT + chunk * D, chunk))
                    for n, ((codes, scales), unit, values, at, g) in enumerate(passes):
                        nc.tensor.matmul_mx(
                            out=accs[i][chunk][:, 2 * x + e, :],
                            lhsT=codes[:, unit * P : (unit + 1) * P].bitcast(FP8X4),
                            lhsT_scale=scales[:, unit * P : (unit + 1) * P],
                            rhs=values[:, at : at + D].bitcast(FP8X4),
                            rhs_scale=near[1][:, V_AT + g * D : V_AT + (g + 1) * D],
                            start=(n == 0),
                            stop=(n == len(passes) - 1),
                        )

        def store(i, chunk):
            h, b = divmod(i, B)
            out_sb = staging.tile([P, 2, 2 * D], F32, name="out_sb")
            copy = nc.vector.tensor_copy if (i, chunk) == (HEADS - 1, 0) else nc.scalar.copy
            copy(
                out=out_sb[:].rearrange("p x e -> p (x e)"),
                in_=accs[i][chunk][:].rearrange("p u d -> p (u d)"),
            )
            rows = out[b, h, chunk * ROWS : (chunk + 1) * ROWS, :].rearrange(
                "(x c a e) d -> a c x (e d)", x=2, a=2, e=2
            )
            for a in range(2):
                nc.sync.dma_start(out=rows[a], in_=out_sb[a * HALF : (a + 1) * HALF, :, :])

        gamma_bf = const.tile([P, H], BF16)
        nc.scalar.dma_start(out=gamma_bf[:], in_=gamma.partition_broadcast(P))
        load(0)
        load(1)
        load(2)

        ln_gamma = const.tile([P, H], F32)
        nc.scalar.activation(out=ln_gamma[:], in_=gamma_bf[:], func=ACT.Ln)

        zeros = const.tile([P, P], BF16)
        nc.vector.memset(zeros[:], 0.0)
        idle = out_psum.tile([P, PACK, P], F32, name="acc0")
        for n in range(WARM_UPS):
            nc.tensor.matmul(
                idle[:, n % PACK, :], lhsT=zeros[:], rhs=zeros[:], start=True, stop=True
            )

        identity = const.tile([P, P], BF16)
        make_identity(nc, identity[:])
        lead = const.tile([P, UNIT + PACK], F32)
        for first, last in ((0, WIDTH), (WIDTH, UNIT + PACK)):
            nc.gpsimd.iota(
                lead[:, first:last],
                pattern=[[1, last - first]],
                base=first,
                channel_multiplier=-PACK,
                allow_small_or_imprecise_dtypes=True,
            )

        near, far = 1 - PACK, ROWS // 2 + 1 - PACK
        offset = [const.tile([P, 2, 2], F32, name="offset%d" % n) for n in range(2)]
        for row, (low, high) in enumerate(((near, far), (far, far), (near, far + ROWS // 2))):
            for p0, value in ((0, low), (HALF, high)):
                engine = nc.vector if row < 2 else nc.gpsimd
                engine.memset(offset[row // 2][p0 : p0 + HALF, row % 2, 0:1], float(value))
                engine.memset(offset[row // 2][p0 : p0 + HALF, row % 2, 1:2], float(-value))

        distance = const.tile([P, TABLE], F32)
        behind = const.tile([P, ROWS_OF_TABLE, WIDTH], F32)

        def distances(rows):
            for row in rows:
                nc.vector.tensor_scalar(
                    out=behind[:, row, :],
                    in0=lead[:, 0:WIDTH],
                    scalar1=offset[row // 2][:, row % 2, 1:2],
                    scalar2=FAR,
                    op0=ALU.is_lt,
                    op1=ALU.mult,
                )
            for row in rows:
                nc.vector.scalar_tensor_tensor(
                    out=distance[:, row * WIDTH : (row + 1) * WIDTH],
                    in0=lead[:, 0:WIDTH],
                    scalar=offset[row // 2][:, row % 2, 0:1],
                    in1=behind[:, row, :],
                    op0=ALU.add,
                    op1=ALU.max,
                )

        nc.vector.tensor_scalar_min(out=ln_gamma[:], in0=ln_gamma[:], scalar1=-1e-25)
        nc.vector.tensor_scalar_add(
            out=distance[:, PAST_AT:TABLE], in0=lead[:], scalar1=float(ROWS + 1 - PACK)
        )
        distances((0, 1, 2))
        padded_k = [const.tile([P, PACK, 4, HALF], BF16, name="padded_k%d" % n) for n in range(3)]
        padded_v = [
            const.tile([P, CHUNKS * D], U32, name="padded_v%d" % n, align_bytes=64) for n in range(2)
        ]
        for tile in padded_k:
            nc.gpsimd.memset(tile[:], 0.0)
        for tile in padded_v:
            nc.gpsimd.memset(tile[:], 0)

        transpose_k(0)
        transpose_q(0)
        decay_table(0, PAST_AT, TABLE)
        copy_k_padded(0)
        decay_table(0, 0, 2 * WIDTH)
        copy_k(0)
        copy_q(0)
        regroup_v(0)
        turn_k(1)
        for n in range(V_BANKS):
            fill_v(n)
        decay_table(0, 2 * WIDTH, 3 * WIDTH)
        shifted_row(0)
        for n in range(2):
            fill_g(n)
            drain_g(n)
        transpose_q(1)

        for i in range(HEADS):
            if i + 3 < HEADS:
                load(i + 3)
            v0, g0 = i * NV, i * NG

            def step(x):
                mask_v(v0 + x)
                fill_v(v0 + x + V_BANKS)

            for j in range(min(NG, 2)):
                mask_g(g0 + j)
            if i > 0:
                if i + 1 < HEADS:
                    regroup_v(i + 1)
                retention(i - 1, 1)
            for x in range(NV):
                if i == 0 and x == 3:
                    copy_q(1)
                step(x)
                if x == (2 if i > 0 else 3):
                    turn_k(i + 2)
                    if i == 0:
                        regroup_v(1)
                        next_table(0)
                if x == 0:
                    fill_g(g0 + 2)
                    drain_g(g0 + 2)
                    mask_g(g0 + 2)
                    if i > 0:
                        next_table(i)
                if x == 4 and i > 0:
                    retention(i - 1, 0)
                    store(i - 1, 0)
                    store(i - 1, 1)
                if x == 6 and i + 2 < HEADS:
                    transpose_q(i + 2)
                    copy_q(i + 2)
            for n in range(g0 + NG, g0 + NG + 2):
                fill_g(n)
                drain_g(n)
            quantise(i, "near")
            if i < HEADS - 1:
                pad_v(i)
                quantise(i, "past")

        i = HEADS - 1
        pad_v(i)
        quantise(i, "past")
        retention(i, 1, (0,))
        retention(i, 0, (0,))
        retention(i, 1, (1,))
        retention(i, 0, (1,))
        store(i, 0)
        store(i, 1)
